import numpy as np
import ml_dtypes


def mxq(x, axis, fmt="e4m3"):
    dtype, down = {"e4m3": (ml_dtypes.float8_e4m3fn, 7), "e5m2": (ml_dtypes.float8_e5m2, 14)}[fmt]
    v = np.moveaxis(np.asarray(x, np.float32).astype(ml_dtypes.bfloat16).astype(np.float64), axis, -1)
    blocks = v.reshape(v.shape[:-1] + (-1, 32))
    amax = np.abs(blocks).max(-1, keepdims=True)
    byte = np.maximum(np.where(amax > 0, np.frexp(amax)[1] - 1 + 127, 0) - down, 1)
    scale = np.exp2(byte - 127.0)
    codes = (blocks / scale).astype(np.float32).astype(dtype).astype(np.float64)
    return np.moveaxis((codes * scale).reshape(v.shape), -1, axis)


WIDE = False


def mx_kscale(k):
    if not WIDE:
        return np.ones(k)
    levels = np.array([10, -10, 5, -5, 0])
    if k % 512:
        return np.exp2(np.random.permutation(np.resize(levels, k // 32))).repeat(32)
    a = np.empty((k // 512, 16))
    for p in range(k // 512):
        a[p, :8] = np.random.permutation(np.resize(levels, 8))
        for g in range(8):
            far = levels[np.abs(levels - a[p, g]) >= 10]
            a[p, g + 8] = far[np.random.randint(len(far))]
    return np.exp2(a.ravel()).repeat(32)


BF16 = ml_dtypes.bfloat16


def bf(x):
    return np.asarray(x, np.float32).astype(BF16)


def f64(x):
    return np.asarray(x).astype(np.float64)


B, F0, FK, S1, S2, D = 64, 64, 128, 128, 128, 16
M1 = F0 * FK
M2 = F0 * S1


def draw0():
    u = mx_kscale(M2).reshape(F0, S1)[:, 0]
    t = mx_kscale(M1).reshape(F0, FK)[0]
    w1 = np.random.standard_normal((F0, FK, S1)) / np.sqrt(M1) / u[:, None, None] / t[None, :, None]
    w2 = np.random.standard_normal((F0, S1, S2)) / np.sqrt(M2) / u[:, None, None]
    return {"x": bf(np.random.standard_normal((B, F0, D)) * u[None, :, None]),
            "x1": bf(np.random.standard_normal((B, FK, D)) * t[None, :, None]),
            "w1": bf(w1.reshape(M1, S1)), "b1": bf(np.random.standard_normal(S1) * 0.2),
            "w2": bf(w2.reshape(M2, S2)), "b2": bf(np.random.standard_normal(S2) * 0.2)}


def core(x, x1, w1, b1, w2, b2):
    x0 = f64(x).transpose(0, 2, 1)
    xk = f64(x1).transpose(0, 2, 1)
    z1 = (x0[:, :, :, None] * xk[:, :, None, :]).reshape(B, D, M1)
    o1 = (mxq(z1, 2, "e4m3") @ mxq(f64(w1), 0, "e4m3")) + f64(b1)
    z2 = (x0[:, :, :, None] * o1[:, :, None, :]).reshape(B, D, M2)
    o2 = (mxq(z2, 2, "e4m3") @ mxq(f64(w2), 0, "e4m3")) + f64(b2)
    return np.concatenate([o1.sum(axis=1), o2.sum(axis=1)], axis=1)


def e4m3fn_bytes(y):
    return np.clip(np.asarray(y, np.float64), -448.0, 448.0).astype(np.float32).astype(ml_dtypes.float8_e4m3fn).view(np.uint8)


def e4m3fn_values(b):
    return np.asarray(b, np.uint8).view(ml_dtypes.float8_e4m3fn).astype(np.float64)


def setup_inputs():
    d = draw0()
    x0 = np.asarray(d['w2']).astype(np.float64)
    s = (np.max(np.abs(x0), axis=(1,), keepdims=True) / 448.0).astype(np.float32)
    out = {}
    for k, v in d.items():
        if k == 'w2':
            out['w2_bytes'] = e4m3fn_bytes(x0 / s.astype(np.float64))
            out['w2_scale'] = s
        else:
            out[k] = v
    return out


def reference(x, x1, w1, b1, w2_bytes, w2_scale, b2):
    return core(x, x1, w1, b1, e4m3fn_values(w2_bytes) * w2_scale.astype(np.float64), b2)

@@ -1,0 +1,283 @@
+from contextlib import ExitStack
+
+import concourse.mybir as mybir
+from concourse.masks import make_identity
+
+F32 = mybir.dt.float32
+BF16 = mybir.dt.bfloat16
+U32 = mybir.dt.uint32
+U8 = mybir.dt.uint8
+FP8 = mybir.dt.float8_e4m3fn
+FP8X4 = mybir.dt.float8_e4m3fn_x4
+MULT = mybir.AluOpType.mult
+ADD = mybir.AluOpType.add
+COPY = mybir.ActivationFunctionType.Copy
+
+FLOPS = 2 * 2 * 1024 * 8192 * 128
+
+P = 128
+TILES = 8
+CHUNKS = 4
+STEPS = TILES * CHUNKS
+LAG = 6
+STEADY = "SGSGSSGSGSSGSGSG"
+TAIL = "VSGVVSVGVSVVGVSV"
+
+
+def tile_cin_pa_kernel(tc, x, x1, w1, b1, w2_bytes, w2_scale, b2, out):
+    nc = tc.nc
+    with ExitStack() as ctx:
+        keep = ctx.enter_context(tc.tile_pool(name="keep", bufs=1))
+        work = ctx.enter_context(tc.tile_pool(name="work", bufs=3))
+        psum = ctx.enter_context(tc.psum_pool(name="psum", bufs=1))
+        ctx.enter_context(tc.manual_schedule())
+
+        xsh = keep.tile([P, 1024], BF16, name="xsh")
+        x1sh = keep.tile([P, 2048], BF16, name="x1sh")
+        xpair = keep.tile([P, TILES, 64, 2], BF16, name="xpair")
+        xs = keep.tile([P, TILES, 64], F32, name="xs")
+        x1w = keep.tile([P, 4, 1024], BF16, name="x1w")
+        xk = keep.tile([P, TILES, 512], BF16, name="xk")
+        ident = keep.tile([P, P], F32, name="ident")
+        sel = keep.tile([P, P], F32, name="sel")
+        b1_row = keep.tile([P, P], BF16, name="b1_row")
+        b2_row = keep.tile([P, P], BF16, name="b2_row")
+        w1_codes = keep.tile([P, 2048], U32, name="w1_codes", align_bytes=64)
+        w1_scales = keep.tile([P, 2048], U8, name="w1_scales", align_bytes=64)
+        w2_codes = keep.tile([P, 2048], U32, name="w2_codes", align_bytes=64)
+        w2_scales = keep.tile([P, 2048], U8, name="w2_scales", align_bytes=64)
+        w2_raw = keep.tile([P, 16, 512], U8, name="w2_raw")
+        w2_sc = keep.tile([P, 64], F32, name="w2_sc")
+        o1 = keep.tile([P, TILES, P], F32, name="o1")
+        fin = keep.tile([P, 256], F32, name="fin")
+        res = keep.tile([P, 256], F32, name="res")
+
+        x_rows = x.rearrange("b i d -> b (i d)")
+        x1_rows = x1.rearrange("b j d -> b (j d)")
+        nc.sync.dma_start(out=xsh[0:64, :], in_=x_rows)
+        nc.scalar.dma_start(out=x1sh[0:64, :], in_=x1_rows)
+        nc.sync.dma_start(out=xsh[64:128, 0:1016], in_=x_rows[:, 8:1024])
+        nc.scalar.dma_start(out=x1sh[64:128, 0:2040], in_=x1_rows[:, 8:2048])
+        w1_view = w1.rearrange("(g p t) n -> p g (t n)", p=P, t=4)
+        w1_raw = []
+        for k in range(4):
+            raw = work.tile([P, 4, 4, P], BF16, name="w1_raw", bufs=4)
+            nc.sync.dma_start(out=raw[:].rearrange("p g t n -> p g (t n)"), in_=w1_view[:, 4 * k : 4 * k + 4, :])
+            w1_raw.append(raw)
+        nc.sync.dma_start(out=w2_sc[:].rearrange("p (g t) -> p g t", t=4), in_=w2_scale.rearrange("(g p t) o -> p g (t o)", p=P, t=4))
+        w2_view = w2_bytes.rearrange("(g p t) n -> p g (t n)", p=P, t=4)
+        for h in range(2):
+            nc.sync.dma_start(out=w2_raw[:, 8 * h : 8 * h + 8, :], in_=w2_view[:, 8 * h : 8 * h + 8, :])
+        nc.sync.dma_start(out=b1_row[:], in_=b1.partition_broadcast(P))
+        nc.sync.dma_start(out=b2_row[:], in_=b2.partition_broadcast(P))
+
+        make_identity(nc, ident[:])
+        nc.gpsimd.memset(sel[:], 0.0)
+        nc.gpsimd.tensor_tensor(out=sel[:, 0:64], in0=ident[:, 0:64], in1=ident[:, 64:128], op=ADD)
+
+        x_dm = xsh[:].rearrange("p (i d) -> p d i", d=16)
+        def make_pairs(t0, t1):
+            nc.vector.tensor_copy(
+                out=xpair[:, t0:t1, :, :],
+                in_=x_dm[:, t0:t1, :].unsqueeze(3).to_broadcast([P, t1 - t0, 64, 2]),
+            )
+        make_pairs(0, 1)
+        nc.vector.tensor_copy(
+            out=x1w[:, 0, :].rearrange("p (j d e) -> p j d e", d=8, e=2),
+            in_=x1sh[:].rearrange("p (j e d) -> p j d e", e=2, d=16)[:, :, 0:8, :],
+        )
+        nc.vector.tensor_copy(out=x1w[:, 2:4, :], in_=x1w[:, 0:1, :].to_broadcast([P, 2, 1024]))
+        nc.scalar.copy(out=x1w[:, 1, :], in_=x1w[:, 0, :])
+
+        x_words = xpair[:].rearrange("p d i e -> p (d i e)").bitcast(F32)
+        x1_words = x1w[:].rearrange("p q c -> p (q c)").bitcast(F32)
+        wide = {}
+        def widen_x(s):
+            t = work.tile([P, 16, 32], F32, name="xrep", bufs=3)
+            nc.vector.tensor_copy(out=t[:], in_=x_words[:, 16 * s : 16 * s + 16].unsqueeze(2).to_broadcast([P, 16, 32]))
+            wide[s] = t
+        x_bank = {}
+        def turn_x(s):
+            bank = psum.tile([P, 4, P], F32, name="x_bank", bufs=2)
+            rows = wide.pop(s)[:].rearrange("p i r -> p (i r)")
+            for g in range(4):
+                nc.tensor.transpose(bank[:, g, :], rows[:, 128 * g : 128 * g + 128], ident[:])
+            x_bank[s] = bank
+        def turn_x1(h):
+            bank = psum.tile([P, 2, 2, P], F32, name="bank", bufs=3)
+            for i in range(2):
+                for u in range(2):
+                    nc.tensor.transpose(bank[:, i, u, :], x1_words[:, 8 * u + 2 * h + i : 2048 : 16], ident[:])
+            nc.scalar.copy(
+                out=xk[:, 2 * h : 2 * h + 2, :].rearrange("p i c -> p (i c)").bitcast(F32).rearrange("p (i c u) -> p i c u", i=2, u=2),
+                in_=bank[:].rearrange("p i u c -> p i c u"),
+            )
+
+        z1_tiles = {}
+        def outer1(s):
+            z1 = work.tile([P, 2048], BF16, name="z1", align_bytes=64, bufs=3)
+            nc.vector.tensor_tensor(
+                out=z1[:].rearrange("p (g c a e) -> p g c a e", g=4, a=2, e=2),
+                in0=x_bank.pop(s)[:].rearrange("p g c -> p (g c)").bitcast(BF16).rearrange("p (g c e) -> p g c e", g=4, e=2).unsqueeze(3).to_broadcast([P, 4, P, 2, 2]),
+                in1=xk[:, s // 4, :].rearrange("p (c a e) -> p c a e", a=2, e=2).unsqueeze(1).to_broadcast([P, 4, P, 2, 2]),
+                op=MULT,
+            )
+            z1_tiles[s] = z1
+        codes1 = {}
+        def quantize1(s):
+            c = work.tile([P, 512], U32, name="z1_codes", align_bytes=64, bufs=4)
+            sc = work.tile([P, 512], U8, name="z1_scales", align_bytes=64, bufs=4)
+            nc.vector.quantize_mx(out=c[:].bitcast(FP8X4), scales=sc[:], in_=z1_tiles.pop(s)[:])
+            codes1[s] = (c, sc)
+
+        def product(acc, codes, s, w_codes, w_scales, first, last):
+            c, sc = codes
+            for g in range(4):
+                cols = slice(128 * g, 128 * g + 128)
+                wcols = slice(128 * (4 * (s % 4) + g), 128 * (4 * (s % 4) + g) + 128)
+                nc.tensor.matmul_mx(
+                    out=acc, lhsT=c[:, cols].bitcast(FP8X4), lhsT_scale=sc[:, cols],
+                    rhs=w_codes[:, wcols].bitcast(FP8X4), rhs_scale=w_scales[:, wcols],
+                    start=(first and g == 0), stop=(last and g == 3),
+                )
+        acc1 = {}
+        def matmul1(s):
+            if s % 4 == 0:
+                acc1[s // 4] = psum.tile([P, P], F32, name="acc1", bufs=2)
+            product(acc1[s // 4][:], codes1.pop(s), s, w1_codes, w1_scales, s % 4 == 0, s % 4 == 3)
+        acc2 = psum.tile([P, P], F32, name="acc2")
+        codes2 = {}
+        def matmul2(m):
+            product(acc2[:], codes2.pop(m), m, w2_codes, w2_scales, m == 0, m == STEPS - 1)
+
+        def leave1(t):
+            nc.vector.tensor_tensor(
+                out=o1[:, t, :].rearrange("p (u m e) -> p u m e", u=2, e=2),
+                in0=acc1.pop(t)[:].rearrange("p (m u e) -> p u m e", u=2, e=2),
+                in1=b1_row[:].rearrange("p (m u e) -> p u m e", u=2, e=2),
+                op=ADD,
+            )
+        def sum1(t):
+            if t > 0:
+                nc.gpsimd.tensor_tensor(out=fin[:, 0:128], in0=(o1[:, 0, :] if t == 1 else fin[:, 0:128]), in1=o1[:, t, :], op=ADD)
+
+        z2_tm = {}
+        def outer2(m, order):
+            z = work.tile([P, 2, 16, 64], BF16, name="z2_tm", bufs=3)
+            src = o1[:, m // 4, :].rearrange("p (u c) -> p u c", u=2)
+            for r in range(16):
+                i = 16 * (m % 4) + r
+                scale = xs[:, m // 4, i : i + 1]
+                if order[r] == "S":
+                    nc.scalar.activation(out=z[:, :, r, :], in_=src, func=COPY, scale=scale)
+                elif order[r] == "V":
+                    nc.vector.tensor_scalar(out=z[:, :, r, :], in0=src, scalar1=scale, scalar2=None, op0=MULT)
+                else:
+                    nc.gpsimd.tensor_scalar(out=z[:, :, r, :], in0=src, scalar1=scale, scalar2=0.0, op0=MULT, op1=ADD)
+            z2_tm[m] = z
+        z2_banks = {}
+        def turn2(m):
+            words = z2_tm.pop(m)[:].rearrange("p u r c -> p (u r c)").bitcast(F32)
+            for h in range(2):
+                bank = psum.tile([P, 2, 2, P], F32, name="bank", bufs=3)
+                for g in range(2):
+                    for u in range(2):
+                        lo = 512 * u + 128 * (2 * h + g)
+                        nc.tensor.transpose(bank[:, g, u, :], words[:, lo : lo + 128], ident[:])
+                z2_banks[m, h] = bank
+        z2_km = {}
+        def leave2(m, engines):
+            z = work.tile([P, 2048], BF16, name="z2_km", align_bytes=64, bufs=3)
+            words = z[:].bitcast(F32).rearrange("p (g c u) -> p g c u", g=4, u=2)
+            for h in range(2):
+                src = z2_banks.pop((m, h))[:].rearrange("p g u c -> p g c u")
+                if engines[h] == "S":
+                    nc.scalar.copy(out=words[:, 2 * h : 2 * h + 2, :, :], in_=src)
+                else:
+                    nc.vector.tensor_copy(out=words[:, 2 * h : 2 * h + 2, :, :], in_=src)
+            z2_km[m] = z
+        def quantize2(m):
+            c = work.tile([P, 512], U32, name="z2_codes", align_bytes=64, bufs=3)
+            sc = work.tile([P, 512], U8, name="z2_scales", align_bytes=64, bufs=3)
+            nc.vector.quantize_mx(out=c[:].bitcast(FP8X4), scales=sc[:], in_=z2_km.pop(m)[:])
+            codes2[m] = (c, sc)
+
+        grouped = {}
+        def interleave(key, raw, engine):
+            g = work.tile([P, 4, P, 4], BF16, name="w_grouped", align_bytes=64, bufs=3)
+            src = raw[:].rearrange("p g t n -> p g n t")
+            if engine == "S":
+                nc.scalar.copy(out=g[:], in_=src)
+            else:
+                nc.vector.tensor_copy(out=g[:], in_=src)
+            grouped[key] = g
+        def quantize_w(key, k, codes, scales):
+            cols = slice(512 * k, 512 * k + 512)
+            nc.vector.quantize_mx(out=codes[:, cols].bitcast(FP8X4), scales=scales[:, cols], in_=grouped.pop(key)[:].rearrange("p g n t -> p (g n t)"))
+        w2_wide = {}
+        def widen_w2(k):
+            w = work.tile([P, 4, 4, P], BF16, name="w2_wide", bufs=3)
+            for g in range(4):
+                for t in range(4):
+                    gg = 4 * k + g
+                    nc.scalar.activation(
+                        out=w[:, g, t, :], in_=w2_raw[:, gg, 128 * t : 128 * t + 128].bitcast(FP8),
+                        func=COPY, scale=w2_sc[:, 4 * gg + t : 4 * gg + t + 1],
+                    )
+            w2_wide[k] = w
+
+        widen_x(0)
+        turn_x(0)
+        make_pairs(1, TILES)
+        widen_x(1)
+        for h in range(4):
+            turn_x1(h)
+        nc.scalar.copy(out=xs[:], in_=x_dm[:, 0:TILES, :])
+
+        W1_ENGINE = "SVSV"
+        for s in range(STEPS + LAG + 4):
+            if s < 4:
+                interleave(("w1", s), w1_raw[s], W1_ENGINE[s])
+            if 2 <= s < 6:
+                widen_w2(s - 2)
+            if s + 2 < STEPS:
+                widen_x(s + 2)
+            if s + 1 < STEPS:
+                turn_x(s + 1)
+            if s < STEPS:
+                outer1(s)
+            if 3 <= s < 7:
+                interleave(("w2", s - 3), w2_wide.pop(s - 3), "V")
+            m = s - LAG
+            if m >= 0 and m % 4 == 0 and m < STEPS:
+                leave1(m // 4)
+            if 0 <= m - 2 < STEPS:
+                quantize2(m - 2)
+            if 1 <= s < 5:
+                quantize_w(("w1", s - 1), s - 1, w1_codes, w1_scales)
+            if 4 <= s < 8:
+                quantize_w(("w2", s - 4), s - 4, w2_codes, w2_scales)
+            if 0 <= m < STEPS:
+                outer2(m, STEADY if s < STEPS + 1 else TAIL)
+            if m >= 0 and m % 4 == 0 and m < STEPS:
+                sum1(m // 4)
+            if 0 <= s - 1 < STEPS:
+                quantize1(s - 1)
+            if 0 <= m - 1 < STEPS:
+                turn2(m - 1)
+                leave2(m - 1, "SS" if s < STEPS + 1 else "VS")
+            if 0 <= s - 2 < STEPS:
+                matmul1(s - 2)
+            if 0 <= m - 3 < STEPS:
+                matmul2(m - 3)
+
+        nc.vector.scalar_tensor_tensor(out=fin[:, 128:256], in0=b2_row[:], scalar=8.0, in1=acc2[:], op0=MULT, op1=ADD)
+        total = psum.tile([P, 2, 2, P], F32, name="bank", bufs=3)
+        tot = total[:].rearrange("p a b c -> p (a b c)")
+        nc.tensor.matmul(tot[:, 0:256], lhsT=sel[:], rhs=fin[:], start=True, stop=True)
+        nc.vector.tensor_copy(
+            out=res[:, 0:128].rearrange("p (m u e) -> p m u e", u=2, e=2),
+            in_=tot[:, 0:128].rearrange("p (u m e) -> p m u e", u=2, e=2),
+        )
+        nc.vector.tensor_copy(out=res[:, 128:256], in_=tot[:, 128:256])
+        nc.sync.dma_start(out=out, in_=res[0:64, :])

@@ -20,8 +20,8 @@ TILES = 8
 CHUNKS = 4
 STEPS = TILES * CHUNKS
 LAG = 6
-STEADY = "SGSGSSGSGSSGSGSG"
-TAIL = "VSGVVSVGVSVVGVSV"
+STEADY = "SSVSSSVSSSVSSSVS"
+TAIL = "VSVVVSVVVSVVVSVV"
 
 
 def tile_cin_pa_kernel(tc, x, x1, w1, b1, w2_bytes, w2_scale, b2, out):

@@ -19,9 +19,19 @@ P = 128
 TILES = 8
 CHUNKS = 4
 STEPS = TILES * CHUNKS
-LAG = 6
-STEADY = "SSVSSSVSSSVSSSVS"
-TAIL = "VSVVVSVVVSVVVSVV"
+LAG = 10
+ML = 5
+W1I = [2,2,3,4]
+W1Q = [3,4,5,6]
+W2W = [2,3,6,6]
+W2I = [5,6,6,8]
+W2Q = [9,10,11,12]
+X1 = [-1,1,3,5]
+ORDERS = ["SSSVSSVSSVSSVSSV","SSSVSSVSSVSSVSSV","SSSVSSVSSVSSVSSV","SSSVSSVSSVSSVSSV","SSSVSSVSSVSSVSSV","SSSVSSVSSVSSVSSV","SSSVSSVSSVSSVSSV","SSSVSSVSSVSSVSSV","SSSVSSVSSVSSVSSV","SSVSSVSVSSVSSVSV","SSVSSVSVSSVSSVSV","SSVSSVSVSSVSSVSV","SSVSSVSVSSVSSVSV","SSSVSSVSSVSSVSSV","SSSVSSVSSVSSVSSV","SSSVSSVSSVSSVSSV","SSSVSSVSSVSSVSSV","SSSVSSVSSVSSVSSV","SSVSSVSVSSVSSVSV","SSVSSVSVSSVSSVSV","SSSVSSVSSVSSVSSV","SSSVSSVSSVSSVSSV","SVVVSVVVSVVVSVVV","SVVVVSVVVVSVVVVV","SVVVVSVVVVSVVVVV","SVVVVSVVVVSVVVVV","SVVVVSVVVVSVVVVV","SVVVSVVVSVVVSVVV","SVVSVVSVVSVVSVVV","SVSVVSVVSVSVVSVV","SVSVVSVVSVSVVSVV","SVSVVSVVSVSVVSVV"]
+EVAC = ["SS","SS","SS","SS","SS","SS","SS","SS","SS","SS","SS","SS","SS","SS","SS","SS","SS","SS","SS","SS","SS","SS","SS","SS","SS","SS","SS","SS","SV","SS","SS","SS"]
+W1_ENGINE = "PPPP"
+W2_ENGINE = "VVPP"
+WARM = 0
 
 
 def tile_cin_pa_kernel(tc, x, x1, w1, b1, w2_bytes, w2_scale, b2, out):
@@ -35,6 +45,7 @@ def tile_cin_pa_kernel(tc, x, x1, w1, b1, w2_bytes, w2_scale, b2, out):
         xsh = keep.tile([P, 1024], BF16, name="xsh")
         x1sh = keep.tile([P, 2048], BF16, name="x1sh")
         xpair = keep.tile([P, TILES, 64, 2], BF16, name="xpair")
+        xt = keep.tile([P, 4, P], F32, name="xt")
         xs = keep.tile([P, TILES, 64], F32, name="xs")
         x1w = keep.tile([P, 4, 1024], BF16, name="x1w")
         xk = keep.tile([P, TILES, 512], BF16, name="xk")
@@ -55,8 +66,8 @@ def tile_cin_pa_kernel(tc, x, x1, w1, b1, w2_bytes, w2_scale, b2, out):
         x_rows = x.rearrange("b i d -> b (i d)")
         x1_rows = x1.rearrange("b j d -> b (j d)")
         nc.sync.dma_start(out=xsh[0:64, :], in_=x_rows)
-        nc.scalar.dma_start(out=x1sh[0:64, :], in_=x1_rows)
-        nc.sync.dma_start(out=xsh[64:128, 0:1016], in_=x_rows[:, 8:1024])
+        nc.scalar.dma_start(out=xsh[64:128, 0:1016], in_=x_rows[:, 8:1024])
+        nc.sync.dma_start(out=x1sh[0:64, :], in_=x1_rows)
         nc.scalar.dma_start(out=x1sh[64:128, 0:2040], in_=x1_rows[:, 8:2048])
         w1_view = w1.rearrange("(g p t) n -> p g (t n)", p=P, t=4)
         w1_raw = []
@@ -64,45 +75,66 @@ def tile_cin_pa_kernel(tc, x, x1, w1, b1, w2_bytes, w2_scale, b2, out):
             raw = work.tile([P, 4, 4, P], BF16, name="w1_raw", bufs=4)
             nc.sync.dma_start(out=raw[:].rearrange("p g t n -> p g (t n)"), in_=w1_view[:, 4 * k : 4 * k + 4, :])
             w1_raw.append(raw)
+
+        make_identity(nc, ident[:])
+        nc.gpsimd.memset(sel[:], 0.0)
+        nc.gpsimd.tensor_tensor(out=sel[:, 0:64], in0=ident[:, 0:64], in1=ident[:, 64:128], op=ADD)
+        ident16 = keep.tile([P, P], BF16, name="ident16")
+        nc.gpsimd.tensor_copy(out=ident16[:], in_=ident[:])
+
+        x_dm = xsh[:].rearrange("p (i d) -> p d i", d=16)
+        xrep = keep.tile([P, 64, 32], F32, name="xrep")
+        x_words = xpair[:].rearrange("p d i e -> p (d i e)").bitcast(F32)
+        def make_pairs(t0, t1):
+            nc.vector.tensor_copy(out=xpair[:, t0:t1, :, :], in_=x_dm[:, t0:t1, :].unsqueeze(3).to_broadcast([P, t1 - t0, 64, 2]))
+        def repeat_x(k):
+            nc.vector.tensor_copy(out=xrep[:, 16 * k : 16 * k + 16, :], in_=x_words[:, 16 * k : 16 * k + 16].unsqueeze(2).to_broadcast([P, 16, 32]))
+        make_pairs(0, 1)
+        repeat_x(0)
+        make_pairs(1, TILES)
+        repeat_x(1)
+        nc.vector.tensor_copy(
+            out=x1w[:, 0, :].rearrange("p (j d e) -> p j d e", d=8, e=2),
+            in_=x1sh[:].rearrange("p (j e d) -> p j d e", e=2, d=16)[:, :, 0:8, :],
+        )
+        nc.vector.tensor_copy(out=x1w[:, 2:4, :], in_=x1w[:, 0:1, :].to_broadcast([P, 2, 1024]))
+        repeat_x(2)
+        repeat_x(3)
+        x1_words = x1w[:].rearrange("p q c -> p (q c)").bitcast(F32)
+        x_bank = {}
+        def turn_x(k):
+            bank = psum.tile([P, 4, P], F32, name="x_bank" if k < 2 else "acc1", bufs=2)
+            rows = xrep[:].rearrange("p i r -> p (i r)")
+            for g in range(4):
+                nc.tensor.transpose(bank[:, g, :], rows[:, 512 * k + 128 * g : 512 * k + 128 * g + 128], ident[:])
+            x_bank[k] = bank
+        turn_x(0)
+        first = psum.tile([P, 4, P], F32, name="bank", bufs=3)
+        for h in range(4):
+            nc.tensor.transpose(first[:, h, :], x_words[:, 128 * h : 128 * h + 128], ident[:])
+        nc.scalar.copy(out=xt[:], in_=first[:])
+
+        scratch = out.rearrange("b (h n) -> (b h) n", h=2)
+        x_view = scratch.rearrange("(d g q) n -> d q g n", d=2, q=4)
+        xb = {}
+        def spread(h):
+            nc.sync.dma_start(out=scratch, in_=xt[:, h, :])
+            for d in range(1 if h == 0 else 0, 2):
+                t = work.tile([P, 16, P], F32, name="xb", bufs=4)
+                for q in range(4):
+                    nc.sync.dma_start(out=t[32 * q : 32 * q + 32, :, :], in_=x_view[d, q].partition_broadcast(32))
+                xb[2 * h + d] = t
+        spread(0)
         nc.sync.dma_start(out=w2_sc[:].rearrange("p (g t) -> p g t", t=4), in_=w2_scale.rearrange("(g p t) o -> p g (t o)", p=P, t=4))
         w2_view = w2_bytes.rearrange("(g p t) n -> p g (t n)", p=P, t=4)
         for h in range(2):
             nc.sync.dma_start(out=w2_raw[:, 8 * h : 8 * h + 8, :], in_=w2_view[:, 8 * h : 8 * h + 8, :])
         nc.sync.dma_start(out=b1_row[:], in_=b1.partition_broadcast(P))
         nc.sync.dma_start(out=b2_row[:], in_=b2.partition_broadcast(P))
+        spread(1)
 
-        make_identity(nc, ident[:])
-        nc.gpsimd.memset(sel[:], 0.0)
-        nc.gpsimd.tensor_tensor(out=sel[:, 0:64], in0=ident[:, 0:64], in1=ident[:, 64:128], op=ADD)
-
-        x_dm = xsh[:].rearrange("p (i d) -> p d i", d=16)
-        def make_pairs(t0, t1):
-            nc.vector.tensor_copy(
-                out=xpair[:, t0:t1, :, :],
-                in_=x_dm[:, t0:t1, :].unsqueeze(3).to_broadcast([P, t1 - t0, 64, 2]),
-            )
-        make_pairs(0, 1)
-        nc.vector.tensor_copy(
-            out=x1w[:, 0, :].rearrange("p (j d e) -> p j d e", d=8, e=2),
-            in_=x1sh[:].rearrange("p (j e d) -> p j d e", e=2, d=16)[:, :, 0:8, :],
-        )
-        nc.vector.tensor_copy(out=x1w[:, 2:4, :], in_=x1w[:, 0:1, :].to_broadcast([P, 2, 1024]))
         nc.scalar.copy(out=x1w[:, 1, :], in_=x1w[:, 0, :])
 
-        x_words = xpair[:].rearrange("p d i e -> p (d i e)").bitcast(F32)
-        x1_words = x1w[:].rearrange("p q c -> p (q c)").bitcast(F32)
-        wide = {}
-        def widen_x(s):
-            t = work.tile([P, 16, 32], F32, name="xrep", bufs=3)
-            nc.vector.tensor_copy(out=t[:], in_=x_words[:, 16 * s : 16 * s + 16].unsqueeze(2).to_broadcast([P, 16, 32]))
-            wide[s] = t
-        x_bank = {}
-        def turn_x(s):
-            bank = psum.tile([P, 4, P], F32, name="x_bank", bufs=2)
-            rows = wide.pop(s)[:].rearrange("p i r -> p (i r)")
-            for g in range(4):
-                nc.tensor.transpose(bank[:, g, :], rows[:, 128 * g : 128 * g + 128], ident[:])
-            x_bank[s] = bank
         def turn_x1(h):
             bank = psum.tile([P, 2, 2, P], F32, name="bank", bufs=3)
             for i in range(2):
@@ -116,17 +148,19 @@ def tile_cin_pa_kernel(tc, x, x1, w1, b1, w2_bytes, w2_scale, b2, out):
         z1_tiles = {}
         def outer1(s):
             z1 = work.tile([P, 2048], BF16, name="z1", align_bytes=64, bufs=3)
+            g = 4 * (s % 4)
+            words = x_bank.pop(s)[:] if s < 4 else xb[s // 4][:, g : g + 4, :]
             nc.vector.tensor_tensor(
                 out=z1[:].rearrange("p (g c a e) -> p g c a e", g=4, a=2, e=2),
-                in0=x_bank.pop(s)[:].rearrange("p g c -> p (g c)").bitcast(BF16).rearrange("p (g c e) -> p g c e", g=4, e=2).unsqueeze(3).to_broadcast([P, 4, P, 2, 2]),
+                in0=words.rearrange("p g c -> p (g c)").bitcast(BF16).rearrange("p (g c e) -> p g c e", g=4, e=2).unsqueeze(3).to_broadcast([P, 4, P, 2, 2]),
                 in1=xk[:, s // 4, :].rearrange("p (c a e) -> p c a e", a=2, e=2).unsqueeze(1).to_broadcast([P, 4, P, 2, 2]),
                 op=MULT,
             )
             z1_tiles[s] = z1
         codes1 = {}
         def quantize1(s):
-            c = work.tile([P, 512], U32, name="z1_codes", align_bytes=64, bufs=4)
-            sc = work.tile([P, 512], U8, name="z1_scales", align_bytes=64, bufs=4)
+            c = work.tile([P, 512], U32, name="z1_codes", align_bytes=64, bufs=8)
+            sc = work.tile([P, 512], U8, name="z1_scales", align_bytes=64, bufs=8)
             nc.vector.quantize_mx(out=c[:].bitcast(FP8X4), scales=sc[:], in_=z1_tiles.pop(s)[:])
             codes1[s] = (c, sc)
 
@@ -148,7 +182,14 @@ def tile_cin_pa_kernel(tc, x, x1, w1, b1, w2_bytes, w2_scale, b2, out):
         acc2 = psum.tile([P, P], F32, name="acc2")
         codes2 = {}
         def matmul2(m):
+            c, sc = codes2[m]
             product(acc2[:], codes2.pop(m), m, w2_codes, w2_scales, m == 0, m == STEPS - 1)
+            for i in range(WARM):
+                dummy = psum.tile([P, 512], F32, name="dummy", bufs=1)
+                nc.tensor.matmul_mx(
+                    out=dummy[:], lhsT=c[:, 0:128].bitcast(FP8X4), lhsT_scale=sc[:, 0:128],
+                    rhs=w2_codes[:, 0:512].bitcast(FP8X4), rhs_scale=w2_scales[:, 0:512], start=True, stop=True,
+                )
 
         def leave1(t):
             nc.vector.tensor_tensor(
@@ -170,10 +211,8 @@ def tile_cin_pa_kernel(tc, x, x1, w1, b1, w2_bytes, w2_scale, b2, out):
                 scale = xs[:, m // 4, i : i + 1]
                 if order[r] == "S":
                     nc.scalar.activation(out=z[:, :, r, :], in_=src, func=COPY, scale=scale)
-                elif order[r] == "V":
-                    nc.vector.tensor_scalar(out=z[:, :, r, :], in0=src, scalar1=scale, scalar2=None, op0=MULT)
                 else:
-                    nc.gpsimd.tensor_scalar(out=z[:, :, r, :], in0=src, scalar1=scale, scalar2=0.0, op0=MULT, op1=ADD)
+                    nc.vector.tensor_scalar(out=z[:, :, r, :], in0=src, scalar1=scale, scalar2=None, op0=MULT)
             z2_tm[m] = z
         z2_banks = {}
         def turn2(m):
@@ -204,19 +243,23 @@ def tile_cin_pa_kernel(tc, x, x1, w1, b1, w2_bytes, w2_scale, b2, out):
 
         grouped = {}
         def interleave(key, raw, engine):
-            g = work.tile([P, 4, P, 4], BF16, name="w_grouped", align_bytes=64, bufs=3)
+            g = work.tile([P, 4, P, 4], BF16, name="w_grouped", align_bytes=64, bufs=6)
             src = raw[:].rearrange("p g t n -> p g n t")
-            if engine == "S":
-                nc.scalar.copy(out=g[:], in_=src)
-            else:
+            if engine == "V":
                 nc.vector.tensor_copy(out=g[:], in_=src)
+            else:
+                for h in range(2):
+                    bank = psum.tile([P, 2, 512], BF16, name="bank", bufs=3)
+                    for i in range(2):
+                        nc.tensor.matmul(bank[:, i, :], lhsT=ident16[:], rhs=src[:, 2 * h + i, :, :], start=True, stop=True)
+                    nc.scalar.copy(out=g[:, 2 * h : 2 * h + 2, :, :].rearrange("p g n t -> p (g n t)"), in_=bank[:].rearrange("p i c -> p (i c)"))
             grouped[key] = g
         def quantize_w(key, k, codes, scales):
             cols = slice(512 * k, 512 * k + 512)
             nc.vector.quantize_mx(out=codes[:, cols].bitcast(FP8X4), scales=scales[:, cols], in_=grouped.pop(key)[:].rearrange("p g n t -> p (g n t)"))
         w2_wide = {}
         def widen_w2(k):
-            w = work.tile([P, 4, 4, P], BF16, name="w2_wide", bufs=3)
+            w = work.tile([P, 4, 4, P], BF16, name="w2_wide", bufs=4)
             for g in range(4):
                 for t in range(4):
                     gg = 4 * k + g
@@ -226,50 +269,54 @@ def tile_cin_pa_kernel(tc, x, x1, w1, b1, w2_bytes, w2_scale, b2, out):
                     )
             w2_wide[k] = w
 
-        widen_x(0)
-        turn_x(0)
-        make_pairs(1, TILES)
-        widen_x(1)
-        for h in range(4):
-            turn_x1(h)
-        nc.scalar.copy(out=xs[:], in_=x_dm[:, 0:TILES, :])
-
-        W1_ENGINE = "SVSV"
-        for s in range(STEPS + LAG + 4):
-            if s < 4:
-                interleave(("w1", s), w1_raw[s], W1_ENGINE[s])
-            if 2 <= s < 6:
-                widen_w2(s - 2)
-            if s + 2 < STEPS:
-                widen_x(s + 2)
-            if s + 1 < STEPS:
-                turn_x(s + 1)
-            if s < STEPS:
-                outer1(s)
-            if 3 <= s < 7:
-                interleave(("w2", s - 3), w2_wide.pop(s - 3), "V")
+        turn_x1(0)
+        for k in range(1, 4):
+            turn_x(k)
+        for s in range(-1, STEPS + LAG + 4):
+            for h in range(1, 4):
+                if X1[h] == s:
+                    turn_x1(h)
+            if s == 2:
+                nc.scalar.copy(out=xs[:], in_=x_dm[:, 0:TILES, :])
+            for k in range(4):
+                if W1I[k] == s:
+                    interleave(("w1", k), w1_raw[k], W1_ENGINE[k])
+            if s in (10, 18):
+                spread(s // 8 + 1)
+            if s < 0:
+                continue
+            for k in range(4):
+                if W2W[k] == s:
+                    widen_w2(k)
             m = s - LAG
-            if m >= 0 and m % 4 == 0 and m < STEPS:
-                leave1(m // 4)
-            if 0 <= m - 2 < STEPS:
-                quantize2(m - 2)
-            if 1 <= s < 5:
-                quantize_w(("w1", s - 1), s - 1, w1_codes, w1_scales)
-            if 4 <= s < 8:
-                quantize_w(("w2", s - 4), s - 4, w2_codes, w2_scales)
-            if 0 <= m < STEPS:
-                outer2(m, STEADY if s < STEPS + 1 else TAIL)
-            if m >= 0 and m % 4 == 0 and m < STEPS:
-                sum1(m // 4)
-            if 0 <= s - 1 < STEPS:
-                quantize1(s - 1)
             if 0 <= m - 1 < STEPS:
                 turn2(m - 1)
-                leave2(m - 1, "SS" if s < STEPS + 1 else "VS")
-            if 0 <= s - 2 < STEPS:
-                matmul1(s - 2)
+            if 0 <= s - ML < STEPS:
+                matmul1(s - ML)
             if 0 <= m - 3 < STEPS:
                 matmul2(m - 3)
+            if s < STEPS:
+                outer1(s)
+            for k in range(4):
+                if W2I[k] == s:
+                    interleave(("w2", k), w2_wide.pop(k), W2_ENGINE[k])
+            if 0 <= m - 2 < STEPS:
+                quantize2(m - 2)
+            for k in range(4):
+                if W1Q[k] == s:
+                    quantize_w(("w1", k), k, w1_codes, w1_scales)
+                if W2Q[k] == s:
+                    quantize_w(("w2", k), k, w2_codes, w2_scales)
+            if 0 <= m < STEPS:
+                outer2(m, ORDERS[m])
+            if 0 <= m - 1 < STEPS:
+                leave2(m - 1, EVAC[m - 1])
+            if s < STEPS:
+                quantize1(s)
+            f = s - ML - 3
+            if f >= 0 and f % 4 == 0 and f < STEPS:
+                leave1(f // 4)
+                sum1(f // 4)
 
         nc.vector.scalar_tensor_tensor(out=fin[:, 128:256], in0=b2_row[:], scalar=8.0, in1=acc2[:], op0=MULT, op1=ADD)
         total = psum.tile([P, 2, 2, P], F32, name="bank", bufs=3)

@@ -21,15 +21,17 @@ CHUNKS = 4
 STEPS = TILES * CHUNKS
 LAG = 10
 ML = 5
-W1I = [2,2,3,4]
-W1Q = [3,4,5,6]
-W2W = [2,3,6,6]
-W2I = [5,6,6,8]
-W2Q = [9,10,11,12]
-X1 = [-1,1,3,5]
-ORDERS = ["SSSVSSVSSVSSVSSV","SSSVSSVSSVSSVSSV","SSSVSSVSSVSSVSSV","SSSVSSVSSVSSVSSV","SSSVSSVSSVSSVSSV","SSSVSSVSSVSSVSSV","SSSVSSVSSVSSVSSV","SSSVSSVSSVSSVSSV","SSSVSSVSSVSSVSSV","SSVSSVSVSSVSSVSV","SSVSSVSVSSVSSVSV","SSVSSVSVSSVSSVSV","SSVSSVSVSSVSSVSV","SSSVSSVSSVSSVSSV","SSSVSSVSSVSSVSSV","SSSVSSVSSVSSVSSV","SSSVSSVSSVSSVSSV","SSSVSSVSSVSSVSSV","SSVSSVSVSSVSSVSV","SSVSSVSVSSVSSVSV","SSSVSSVSSVSSVSSV","SSSVSSVSSVSSVSSV","SVVVSVVVSVVVSVVV","SVVVVSVVVVSVVVVV","SVVVVSVVVVSVVVVV","SVVVVSVVVVSVVVVV","SVVVVSVVVVSVVVVV","SVVVSVVVSVVVSVVV","SVVSVVSVVSVVSVVV","SVSVVSVVSVSVVSVV","SVSVVSVVSVSVVSVV","SVSVVSVVSVSVVSVV"]
+WFIRST = True
+SPREAD = {2: 3, 8: 4, 12: 5, 16: 6, 20: 7}
+W1I = [0,2,2,4]
+W1Q = [3,5,6,7]
+W2W = [0,0,4,6]
+W2I = [5,5,7,8]
+W2Q = [8,9,10,11]
+X1 = [-1,0,1,5]
+ORDERS = ["SSSVSSVSSVSSVSSV","SSSVSSVSSVSSVSSV","SSSVSSVSSVSSVSSV","SSSVSSVSSVSSVSSV","SSSVSSVSSVSSVSSV","SSVSSVSVSSVSSVSV","SSSVSSVSSVSSVSSV","SSVSSVSVSSVSSVSV","SSSVSSVSSVSSVSSV","SSVSSVSVSSVSSVSV","SSVSSVSVSSVSSVSV","SSVSSVSVSSVSSVSV","SSVSSVSVSSVSSVSV","SSSVSSVSSVSSVSSV","SSSVSSVSSVSSVSSV","SSVSSVSVSSVSSVSV","SSVSSVSVSSVSSVSV","SSVSSVSVSSVSSVSV","SVSVSVSVSVSVSVSV","SSVSVSVSSVSVSVSV","SSVSSVSVSSVSSVSV","SSVSVSVSSVSVSVSV","SVVVVVVVSVVVVVVV","SVVVVSVVVVSVVVVV","SVVVVSVVVVSVVVVV","SVVVVSVVVVSVVVVV","SVVVSVVVSVVVSVVV","SVVSVVSVVSVVSVVV","SVVSVVSVVSVVSVVV","SVSVSVSVVSVSVSVV","SVVVSVVVSVVVSVVV","SVVVSVVVSVVVSVVV"]
 EVAC = ["SS","SS","SS","SS","SS","SS","SS","SS","SS","SS","SS","SS","SS","SS","SS","SS","SS","SS","SS","SS","SS","SS","SS","SS","SS","SS","SS","SS","SV","SS","SS","SS"]
-W1_ENGINE = "PPPP"
+W1_ENGINE = "VPPP"
 W2_ENGINE = "VVPP"
 WARM = 0
 
@@ -45,7 +47,7 @@ def tile_cin_pa_kernel(tc, x, x1, w1, b1, w2_bytes, w2_scale, b2, out):
         xsh = keep.tile([P, 1024], BF16, name="xsh")
         x1sh = keep.tile([P, 2048], BF16, name="x1sh")
         xpair = keep.tile([P, TILES, 64, 2], BF16, name="xpair")
-        xt = keep.tile([P, 4, P], F32, name="xt")
+        xt = keep.tile([P, 4, P, 2], F32, name="xt")
         xs = keep.tile([P, TILES, 64], F32, name="xs")
         x1w = keep.tile([P, 4, 1024], BF16, name="x1w")
         xk = keep.tile([P, TILES, 512], BF16, name="xk")
@@ -65,16 +67,22 @@ def tile_cin_pa_kernel(tc, x, x1, w1, b1, w2_bytes, w2_scale, b2, out):
 
         x_rows = x.rearrange("b i d -> b (i d)")
         x1_rows = x1.rearrange("b j d -> b (j d)")
-        nc.sync.dma_start(out=xsh[0:64, :], in_=x_rows)
-        nc.scalar.dma_start(out=xsh[64:128, 0:1016], in_=x_rows[:, 8:1024])
         nc.sync.dma_start(out=x1sh[0:64, :], in_=x1_rows)
         nc.scalar.dma_start(out=x1sh[64:128, 0:2040], in_=x1_rows[:, 8:2048])
+        nc.sync.dma_start(out=xsh[0:64, :], in_=x_rows)
+        nc.scalar.dma_start(out=xsh[64:128, 0:1016], in_=x_rows[:, 8:1024])
         w1_view = w1.rearrange("(g p t) n -> p g (t n)", p=P, t=4)
+        w2_view = w2_bytes.rearrange("(g p t) n -> p g (t n)", p=P, t=4)
         w1_raw = []
-        for k in range(4):
+        def load_w1(k):
             raw = work.tile([P, 4, 4, P], BF16, name="w1_raw", bufs=4)
             nc.sync.dma_start(out=raw[:].rearrange("p g t n -> p g (t n)"), in_=w1_view[:, 4 * k : 4 * k + 4, :])
             w1_raw.append(raw)
+        def load_w2(h):
+            nc.sync.dma_start(out=w2_raw[:, 8 * h : 8 * h + 8, :], in_=w2_view[:, 8 * h : 8 * h + 8, :])
+        load_w1(0)
+        nc.sync.dma_start(out=w2_sc[:].rearrange("p (g t) -> p g t", t=4), in_=w2_scale.rearrange("(g p t) o -> p g (t o)", p=P, t=4))
+        load_w2(0)
 
         make_identity(nc, ident[:])
         nc.gpsimd.memset(sel[:], 0.0)
@@ -83,21 +91,22 @@ def tile_cin_pa_kernel(tc, x, x1, w1, b1, w2_bytes, w2_scale, b2, out):
         nc.gpsimd.tensor_copy(out=ident16[:], in_=ident[:])
 
         x_dm = xsh[:].rearrange("p (i d) -> p d i", d=16)
-        xrep = keep.tile([P, 64, 32], F32, name="xrep")
+        xrep = work.tile([P, 64, 32], F32, name="xb", bufs=6)
         x_words = xpair[:].rearrange("p d i e -> p (d i e)").bitcast(F32)
         def make_pairs(t0, t1):
             nc.vector.tensor_copy(out=xpair[:, t0:t1, :, :], in_=x_dm[:, t0:t1, :].unsqueeze(3).to_broadcast([P, t1 - t0, 64, 2]))
         def repeat_x(k):
             nc.vector.tensor_copy(out=xrep[:, 16 * k : 16 * k + 16, :], in_=x_words[:, 16 * k : 16 * k + 16].unsqueeze(2).to_broadcast([P, 16, 32]))
-        make_pairs(0, 1)
-        repeat_x(0)
-        make_pairs(1, TILES)
-        repeat_x(1)
         nc.vector.tensor_copy(
             out=x1w[:, 0, :].rearrange("p (j d e) -> p j d e", d=8, e=2),
             in_=x1sh[:].rearrange("p (j e d) -> p j d e", e=2, d=16)[:, :, 0:8, :],
         )
+        nc.scalar.copy(out=x1w[:, 1, :], in_=x1w[:, 0, :])
         nc.vector.tensor_copy(out=x1w[:, 2:4, :], in_=x1w[:, 0:1, :].to_broadcast([P, 2, 1024]))
+        make_pairs(0, 1)
+        repeat_x(0)
+        make_pairs(1, TILES)
+        repeat_x(1)
         repeat_x(2)
         repeat_x(3)
         x1_words = x1w[:].rearrange("p q c -> p (q c)").bitcast(F32)
@@ -108,48 +117,59 @@ def tile_cin_pa_kernel(tc, x, x1, w1, b1, w2_bytes, w2_scale, b2, out):
             for g in range(4):
                 nc.tensor.transpose(bank[:, g, :], rows[:, 512 * k + 128 * g : 512 * k + 128 * g + 128], ident[:])
             x_bank[k] = bank
+        def turn_x1(t, n):
+            bank = psum.tile([P, 2, 2, P], F32, name="bank", bufs=3)
+            for i in range(n):
+                for u in range(2):
+                    nc.tensor.transpose(bank[:, i, u, :], x1_words[:, 8 * u + t + i : 2048 : 16], ident[:])
+            nc.scalar.copy(
+                out=xk[:, t : t + n, :].rearrange("p i c -> p (i c)").bitcast(F32).rearrange("p (i c u) -> p i c u", i=n, u=2),
+                in_=bank[:, 0:n, :, :].rearrange("p i u c -> p i c u"),
+            )
+        turn_x1(0, 1)
         turn_x(0)
         first = psum.tile([P, 4, P], F32, name="bank", bufs=3)
         for h in range(4):
             nc.tensor.transpose(first[:, h, :], x_words[:, 128 * h : 128 * h + 128], ident[:])
-        nc.scalar.copy(out=xt[:], in_=first[:])
-
-        scratch = out.rearrange("b (h n) -> (b h) n", h=2)
-        x_view = scratch.rearrange("(d g q) n -> d q g n", d=2, q=4)
+        for h0, h1 in ((0, 1), (1, 4)):
+            nc.scalar.copy(out=xt[:, h0:h1, :, :], in_=first[:, h0:h1, :].unsqueeze(3).to_broadcast([P, h1 - h0, P, 2]))
+        x_view = out.rearrange("(g q) n -> q g n", q=4)
         xb = {}
-        def spread(h):
-            nc.sync.dma_start(out=scratch, in_=xt[:, h, :])
-            for d in range(1 if h == 0 else 0, 2):
-                t = work.tile([P, 16, P], F32, name="xb", bufs=4)
-                for q in range(4):
-                    nc.sync.dma_start(out=t[32 * q : 32 * q + 32, :, :], in_=x_view[d, q].partition_broadcast(32))
-                xb[2 * h + d] = t
-        spread(0)
-        nc.sync.dma_start(out=w2_sc[:].rearrange("p (g t) -> p g t", t=4), in_=w2_scale.rearrange("(g p t) o -> p g (t o)", p=P, t=4))
-        w2_view = w2_bytes.rearrange("(g p t) n -> p g (t n)", p=P, t=4)
-        for h in range(2):
-            nc.sync.dma_start(out=w2_raw[:, 8 * h : 8 * h + 8, :], in_=w2_view[:, 8 * h : 8 * h + 8, :])
+        def spread(t):
+            d = 64 * (t % 2)
+            nc.sync.dma_start(out=out, in_=xt[d : d + 64, t // 2, :, :].rearrange("p c e -> p (c e)"))
+            for h in range(2):
+                if not (t == 1 and h == 1):
+                    spread_half(t, h)
+        def spread_half(t, h):
+            b = work.tile([P, 8, 256], F32, name="xb", bufs=6)
+            for q in range(4):
+                nc.sync.dma_start(out=b[32 * q : 32 * q + 32, :, :], in_=x_view[q, 8 * h : 8 * h + 8, :].partition_broadcast(32))
+            xb[t, h] = b
+        spread(1)
+        load_w1(1)
+        spread_half(1, 1)
+        for k in range(2, 4):
+            load_w1(k)
+        load_w2(1)
         nc.sync.dma_start(out=b1_row[:], in_=b1.partition_broadcast(P))
         nc.sync.dma_start(out=b2_row[:], in_=b2.partition_broadcast(P))
-        spread(1)
-
-        nc.scalar.copy(out=x1w[:, 1, :], in_=x1w[:, 0, :])
-
-        def turn_x1(h):
-            bank = psum.tile([P, 2, 2, P], F32, name="bank", bufs=3)
-            for i in range(2):
-                for u in range(2):
-                    nc.tensor.transpose(bank[:, i, u, :], x1_words[:, 8 * u + 2 * h + i : 2048 : 16], ident[:])
-            nc.scalar.copy(
-                out=xk[:, 2 * h : 2 * h + 2, :].rearrange("p i c -> p (i c)").bitcast(F32).rearrange("p (i c u) -> p i c u", i=2, u=2),
-                in_=bank[:].rearrange("p i u c -> p i c u"),
-            )
+        spread(2)
 
         z1_tiles = {}
         def outer1(s):
             z1 = work.tile([P, 2048], BF16, name="z1", align_bytes=64, bufs=3)
             g = 4 * (s % 4)
-            words = x_bank.pop(s)[:] if s < 4 else xb[s // 4][:, g : g + 4, :]
+            if s >= 4:
+                nc.vector.tensor_tensor(
+                    out=z1[:].rearrange("p (g c) -> p g c", g=4),
+                    in0=xb[s // 4, s % 4 // 2][:, g % 8 : g % 8 + 4, :].rearrange("p g c -> p (g c)").bitcast(BF16).rearrange("p (g c) -> p g c", g=4),
+                    in1=xk[:, s // 4, :].unsqueeze(1).to_broadcast([P, 4, 512]),
+                    op=MULT,
+                )
+                z1_tiles[s] = z1
+                return
+            words = x_bank.pop(s)[:]
             nc.vector.tensor_tensor(
                 out=z1[:].rearrange("p (g c a e) -> p g c a e", g=4, a=2, e=2),
                 in0=words.rearrange("p g c -> p (g c)").bitcast(BF16).rearrange("p (g c e) -> p g c e", g=4, e=2).unsqueeze(3).to_broadcast([P, 4, P, 2, 2]),
@@ -159,8 +179,8 @@ def tile_cin_pa_kernel(tc, x, x1, w1, b1, w2_bytes, w2_scale, b2, out):
             z1_tiles[s] = z1
         codes1 = {}
         def quantize1(s):
-            c = work.tile([P, 512], U32, name="z1_codes", align_bytes=64, bufs=8)
-            sc = work.tile([P, 512], U8, name="z1_scales", align_bytes=64, bufs=8)
+            c = work.tile([P, 512], U32, name="z1_codes", align_bytes=64, bufs=7)
+            sc = work.tile([P, 512], U8, name="z1_scales", align_bytes=64, bufs=7)
             nc.vector.quantize_mx(out=c[:].bitcast(FP8X4), scales=sc[:], in_=z1_tiles.pop(s)[:])
             codes1[s] = (c, sc)
 
@@ -201,6 +221,21 @@ def tile_cin_pa_kernel(tc, x, x1, w1, b1, w2_bytes, w2_scale, b2, out):
         def sum1(t):
             if t > 0:
                 nc.gpsimd.tensor_tensor(out=fin[:, 0:128], in0=(o1[:, 0, :] if t == 1 else fin[:, 0:128]), in1=o1[:, t, :], op=ADD)
+
+        def finish(h):
+            cols = slice(128 * h, 128 * h + 128)
+            if h == 1:
+                nc.vector.scalar_tensor_tensor(out=fin[:, cols], in0=b2_row[:], scalar=8.0, in1=acc2[:], op0=MULT, op1=ADD)
+            total = psum.tile([P, P], F32, name="bank", bufs=3)
+            nc.tensor.matmul(total[:], lhsT=sel[:], rhs=fin[:, cols], start=True, stop=True)
+            if h == 0:
+                nc.scalar.copy(
+                    out=res[:, cols].rearrange("p (m u e) -> p m u e", u=2, e=2),
+                    in_=total[:].rearrange("p (u m e) -> p m u e", u=2, e=2),
+                )
+            else:
+                nc.vector.tensor_copy(out=res[:, cols], in_=total[:])
+            nc.sync.dma_start(out=out[:, cols], in_=res[0:64, cols])
 
         z2_tm = {}
         def outer2(m, order):
@@ -243,7 +278,7 @@ def tile_cin_pa_kernel(tc, x, x1, w1, b1, w2_bytes, w2_scale, b2, out):
 
         grouped = {}
         def interleave(key, raw, engine):
-            g = work.tile([P, 4, P, 4], BF16, name="w_grouped", align_bytes=64, bufs=6)
+            g = work.tile([P, 4, P, 4], BF16, name="w_grouped", align_bytes=64, bufs=5)
             src = raw[:].rearrange("p g t n -> p g n t")
             if engine == "V":
                 nc.vector.tensor_copy(out=g[:], in_=src)
@@ -259,7 +294,7 @@ def tile_cin_pa_kernel(tc, x, x1, w1, b1, w2_bytes, w2_scale, b2, out):
             nc.vector.quantize_mx(out=codes[:, cols].bitcast(FP8X4), scales=scales[:, cols], in_=grouped.pop(key)[:].rearrange("p g n t -> p (g n t)"))
         w2_wide = {}
         def widen_w2(k):
-            w = work.tile([P, 4, 4, P], BF16, name="w2_wide", bufs=4)
+            w = work.tile([P, 4, 4, P], BF16, name="w2_wide", bufs=3)
             for g in range(4):
                 for t in range(4):
                     gg = 4 * k + g
@@ -269,25 +304,30 @@ def tile_cin_pa_kernel(tc, x, x1, w1, b1, w2_bytes, w2_scale, b2, out):
                     )
             w2_wide[k] = w
 
-        turn_x1(0)
+        turn_x1(1, 1)
         for k in range(1, 4):
             turn_x(k)
         for s in range(-1, STEPS + LAG + 4):
             for h in range(1, 4):
                 if X1[h] == s:
-                    turn_x1(h)
+                    turn_x1(2 * h, 2)
             if s == 2:
                 nc.scalar.copy(out=xs[:], in_=x_dm[:, 0:TILES, :])
-            for k in range(4):
-                if W1I[k] == s:
-                    interleave(("w1", k), w1_raw[k], W1_ENGINE[k])
-            if s in (10, 18):
-                spread(s // 8 + 1)
-            if s < 0:
-                continue
+            if not WFIRST:
+                for k in range(4):
+                    if W1I[k] == s:
+                        interleave(("w1", k), w1_raw[k], W1_ENGINE[k])
+            if s in SPREAD:
+                spread(SPREAD[s])
             for k in range(4):
                 if W2W[k] == s:
                     widen_w2(k)
+            if WFIRST:
+                for k in range(4):
+                    if W1I[k] == s:
+                        interleave(("w1", k), w1_raw[k], W1_ENGINE[k])
+            if s < 0:
+                continue
             m = s - LAG
             if 0 <= m - 1 < STEPS:
                 turn2(m - 1)
@@ -317,14 +357,7 @@ def tile_cin_pa_kernel(tc, x, x1, w1, b1, w2_bytes, w2_scale, b2, out):
             if f >= 0 and f % 4 == 0 and f < STEPS:
                 leave1(f // 4)
                 sum1(f // 4)
+            if s == STEPS + ML + 3:
+                finish(0)
 
-        nc.vector.scalar_tensor_tensor(out=fin[:, 128:256], in0=b2_row[:], scalar=8.0, in1=acc2[:], op0=MULT, op1=ADD)
-        total = psum.tile([P, 2, 2, P], F32, name="bank", bufs=3)
-        tot = total[:].rearrange("p a b c -> p (a b c)")
-        nc.tensor.matmul(tot[:, 0:256], lhsT=sel[:], rhs=fin[:], start=True, stop=True)
-        nc.vector.tensor_copy(
-            out=res[:, 0:128].rearrange("p (m u e) -> p m u e", u=2, e=2),
-            in_=tot[:, 0:128].rearrange("p (u m e) -> p m u e", u=2, e=2),
-        )
-        nc.vector.tensor_copy(out=res[:, 128:256], in_=tot[:, 128:256])
-        nc.sync.dma_start(out=out, in_=res[0:64, :])
+        finish(1)

@@ -13,27 +13,33 @@ MULT = mybir.AluOpType.mult
 ADD = mybir.AluOpType.add
 COPY = mybir.ActivationFunctionType.Copy
 
+P = 128
+D = 16
+FIELDS = 64
+TILES = 8
+CHUNK = 2048
+CHUNKS = TILES * 4
+
 FLOPS = 2 * 2 * 1024 * 8192 * 128
 
-P = 128
-TILES = 8
-CHUNKS = 4
-STEPS = TILES * CHUNKS
-LAG = 10
-ML = 5
-WFIRST = True
-SPREAD = {2: 3, 8: 4, 12: 5, 16: 6, 20: 7}
-W1I = [0,2,2,4]
-W1Q = [3,5,6,7]
-W2W = [0,0,4,6]
-W2I = [5,5,7,8]
-W2Q = [8,9,10,11]
-X1 = [-1,0,1,5]
-ORDERS = ["SSSVSSVSSVSSVSSV","SSSVSSVSSVSSVSSV","SSSVSSVSSVSSVSSV","SSSVSSVSSVSSVSSV","SSSVSSVSSVSSVSSV","SSVSSVSVSSVSSVSV","SSSVSSVSSVSSVSSV","SSVSSVSVSSVSSVSV","SSSVSSVSSVSSVSSV","SSVSSVSVSSVSSVSV","SSVSSVSVSSVSSVSV","SSVSSVSVSSVSSVSV","SSVSSVSVSSVSSVSV","SSSVSSVSSVSSVSSV","SSSVSSVSSVSSVSSV","SSVSSVSVSSVSSVSV","SSVSSVSVSSVSSVSV","SSVSSVSVSSVSSVSV","SVSVSVSVSVSVSVSV","SSVSVSVSSVSVSVSV","SSVSSVSVSSVSSVSV","SSVSVSVSSVSVSVSV","SVVVVVVVSVVVVVVV","SVVVVSVVVVSVVVVV","SVVVVSVVVVSVVVVV","SVVVVSVVVVSVVVVV","SVVVSVVVSVVVSVVV","SVVSVVSVVSVVSVVV","SVVSVVSVVSVVSVVV","SVSVSVSVVSVSVSVV","SVVVSVVVSVVVSVVV","SVVVSVVVSVVVSVVV"]
-EVAC = ["SS","SS","SS","SS","SS","SS","SS","SS","SS","SS","SS","SS","SS","SS","SS","SS","SS","SS","SS","SS","SS","SS","SS","SS","SS","SS","SS","SS","SV","SS","SS","SS"]
-W1_ENGINE = "VPPP"
-W2_ENGINE = "VVPP"
-WARM = 0
+MATMUL1_LAG = 5
+Z2_LAG = 10
+
+W1_GROUP_STEP = (0, 1, 1, 5)
+W1_GROUP_ENGINE = ("vector", "scalar", "scalar", "tensor")
+W1_QUANTIZE_STEP = (3, 5, 6, 7)
+W2_WIDEN_STEP = (1, 1, 3, 6)
+W2_GROUP_STEP = (2, 4, 7, 8)
+W2_GROUP_ENGINE = ("vector", "vector", "tensor", "tensor")
+W2_QUANTIZE_STEP = (8, 9, 9, 13)
+X1_TURN_STEP = (-1, 2, 7)
+X_PARK_STEP = (1, 9, 17)
+
+
+def vector_products(m):
+    if m < 8:
+        return 6
+    return 5 if m + Z2_LAG < CHUNKS else 12
 
 
 def tile_cin_pa_kernel(tc, x, x1, w1, b1, w2_bytes, w2_scale, b2, out):
@@ -44,320 +50,361 @@ def tile_cin_pa_kernel(tc, x, x1, w1, b1, w2_bytes, w2_scale, b2, out):
         psum = ctx.enter_context(tc.psum_pool(name="psum", bufs=1))
         ctx.enter_context(tc.manual_schedule())
 
-        xsh = keep.tile([P, 1024], BF16, name="xsh")
-        x1sh = keep.tile([P, 2048], BF16, name="x1sh")
-        xpair = keep.tile([P, TILES, 64, 2], BF16, name="xpair")
-        xt = keep.tile([P, 4, P, 2], F32, name="xt")
-        xs = keep.tile([P, TILES, 64], F32, name="xs")
-        x1w = keep.tile([P, 4, 1024], BF16, name="x1w")
-        xk = keep.tile([P, TILES, 512], BF16, name="xk")
+        x_tok = keep.tile([P, FIELDS * D], BF16, name="x_tok")
+        x1_tok = keep.tile([P, P * D], BF16, name="x1_tok")
+        x_pairs = keep.tile([P, TILES, FIELDS, 2], BF16, name="x_pairs")
+        x_wide = keep.tile([P, FIELDS, 32], F32, name="x_wide")
+        x_turned = keep.tile([P, 4, P], F32, name="x_turned")
+        x_scale = keep.tile([P, TILES, FIELDS], F32, name="x_scale")
+        x1_four = keep.tile([P, 4, 1024], BF16, name="x1_four")
+        x1_by_k = keep.tile([P, TILES, 512], BF16, name="x1_by_k")
         ident = keep.tile([P, P], F32, name="ident")
-        sel = keep.tile([P, P], F32, name="sel")
+        ident16 = keep.tile([P, P], BF16, name="ident16")
+        fold = keep.tile([P, P], F32, name="fold")
         b1_row = keep.tile([P, P], BF16, name="b1_row")
         b2_row = keep.tile([P, P], BF16, name="b2_row")
-        w1_codes = keep.tile([P, 2048], U32, name="w1_codes", align_bytes=64)
-        w1_scales = keep.tile([P, 2048], U8, name="w1_scales", align_bytes=64)
-        w2_codes = keep.tile([P, 2048], U32, name="w2_codes", align_bytes=64)
-        w2_scales = keep.tile([P, 2048], U8, name="w2_scales", align_bytes=64)
-        w2_raw = keep.tile([P, 16, 512], U8, name="w2_raw")
-        w2_sc = keep.tile([P, 64], F32, name="w2_sc")
+        w2_codes8 = keep.tile([P, 16, 512], U8, name="w2_codes8")
+        w2_scales32 = keep.tile([P, 64], F32, name="w2_scales32")
+        w1_codes = keep.tile([P, 16 * P], U32, name="w1_codes", align_bytes=64)
+        w1_scales = keep.tile([P, 16 * P], U8, name="w1_scales", align_bytes=64)
+        w2_codes = keep.tile([P, 16 * P], U32, name="w2_codes", align_bytes=64)
+        w2_scales = keep.tile([P, 16 * P], U8, name="w2_scales", align_bytes=64)
         o1 = keep.tile([P, TILES, P], F32, name="o1")
-        fin = keep.tile([P, 256], F32, name="fin")
-        res = keep.tile([P, 256], F32, name="res")
+        sums = keep.tile([P, 2 * P], F32, name="sums")
+        result = keep.tile([P, 2 * P], F32, name="result")
 
         x_rows = x.rearrange("b i d -> b (i d)")
         x1_rows = x1.rearrange("b j d -> b (j d)")
-        nc.sync.dma_start(out=x1sh[0:64, :], in_=x1_rows)
-        nc.scalar.dma_start(out=x1sh[64:128, 0:2040], in_=x1_rows[:, 8:2048])
-        nc.sync.dma_start(out=xsh[0:64, :], in_=x_rows)
-        nc.scalar.dma_start(out=xsh[64:128, 0:1016], in_=x_rows[:, 8:1024])
+        nc.sync.dma_start(out=x1_tok[0:64, :], in_=x1_rows)
+        nc.scalar.dma_start(out=x1_tok[64:128, 0 : P * D - 8], in_=x1_rows[:, 8 : P * D])
+        nc.sync.dma_start(out=x_tok[0:64, :], in_=x_rows)
+        nc.scalar.dma_start(out=x_tok[64:128, 0 : FIELDS * D - 8], in_=x_rows[:, 8 : FIELDS * D])
+
         w1_view = w1.rearrange("(g p t) n -> p g (t n)", p=P, t=4)
         w2_view = w2_bytes.rearrange("(g p t) n -> p g (t n)", p=P, t=4)
         w1_raw = []
-        def load_w1(k):
+
+        def load_w1(n):
             raw = work.tile([P, 4, 4, P], BF16, name="w1_raw", bufs=4)
-            nc.sync.dma_start(out=raw[:].rearrange("p g t n -> p g (t n)"), in_=w1_view[:, 4 * k : 4 * k + 4, :])
+            nc.sync.dma_start(out=raw[:].rearrange("p g t n -> p g (t n)"), in_=w1_view[:, 4 * n : 4 * n + 4, :])
             w1_raw.append(raw)
-        def load_w2(h):
-            nc.sync.dma_start(out=w2_raw[:, 8 * h : 8 * h + 8, :], in_=w2_view[:, 8 * h : 8 * h + 8, :])
+
+        def load_w2(half):
+            passes = slice(8 * half, 8 * half + 8)
+            nc.sync.dma_start(out=w2_codes8[:, passes, :], in_=w2_view[:, passes, :])
+
         load_w1(0)
-        nc.sync.dma_start(out=w2_sc[:].rearrange("p (g t) -> p g t", t=4), in_=w2_scale.rearrange("(g p t) o -> p g (t o)", p=P, t=4))
+        nc.sync.dma_start(
+            out=w2_scales32[:].rearrange("p (g t) -> p g t", t=4),
+            in_=w2_scale.rearrange("(g p t) o -> p g (t o)", p=P, t=4),
+        )
         load_w2(0)
 
         make_identity(nc, ident[:])
-        nc.gpsimd.memset(sel[:], 0.0)
-        nc.gpsimd.tensor_tensor(out=sel[:, 0:64], in0=ident[:, 0:64], in1=ident[:, 64:128], op=ADD)
-        ident16 = keep.tile([P, P], BF16, name="ident16")
+        nc.gpsimd.memset(fold[:], 0.0)
+        nc.gpsimd.tensor_tensor(out=fold[:, 0:64], in0=ident[:, 0:64], in1=ident[:, 64:128], op=ADD)
         nc.gpsimd.tensor_copy(out=ident16[:], in_=ident[:])
 
-        x_dm = xsh[:].rearrange("p (i d) -> p d i", d=16)
-        xrep = work.tile([P, 64, 32], F32, name="xb", bufs=6)
-        x_words = xpair[:].rearrange("p d i e -> p (d i e)").bitcast(F32)
-        def make_pairs(t0, t1):
-            nc.vector.tensor_copy(out=xpair[:, t0:t1, :, :], in_=x_dm[:, t0:t1, :].unsqueeze(3).to_broadcast([P, t1 - t0, 64, 2]))
-        def repeat_x(k):
-            nc.vector.tensor_copy(out=xrep[:, 16 * k : 16 * k + 16, :], in_=x_words[:, 16 * k : 16 * k + 16].unsqueeze(2).to_broadcast([P, 16, 32]))
-        nc.vector.tensor_copy(
-            out=x1w[:, 0, :].rearrange("p (j d e) -> p j d e", d=8, e=2),
-            in_=x1sh[:].rearrange("p (j e d) -> p j d e", e=2, d=16)[:, :, 0:8, :],
-        )
-        nc.scalar.copy(out=x1w[:, 1, :], in_=x1w[:, 0, :])
-        nc.vector.tensor_copy(out=x1w[:, 2:4, :], in_=x1w[:, 0:1, :].to_broadcast([P, 2, 1024]))
-        make_pairs(0, 1)
-        repeat_x(0)
-        make_pairs(1, TILES)
-        repeat_x(1)
-        repeat_x(2)
-        repeat_x(3)
-        x1_words = x1w[:].rearrange("p q c -> p (q c)").bitcast(F32)
-        x_bank = {}
-        def turn_x(k):
-            bank = psum.tile([P, 4, P], F32, name="x_bank" if k < 2 else "acc1", bufs=2)
-            rows = xrep[:].rearrange("p i r -> p (i r)")
-            for g in range(4):
-                nc.tensor.transpose(bank[:, g, :], rows[:, 512 * k + 128 * g : 512 * k + 128 * g + 128], ident[:])
-            x_bank[k] = bank
-        def turn_x1(t, n):
-            bank = psum.tile([P, 2, 2, P], F32, name="bank", bufs=3)
-            for i in range(n):
-                for u in range(2):
-                    nc.tensor.transpose(bank[:, i, u, :], x1_words[:, 8 * u + t + i : 2048 : 16], ident[:])
-            nc.scalar.copy(
-                out=xk[:, t : t + n, :].rearrange("p i c -> p (i c)").bitcast(F32).rearrange("p (i c u) -> p i c u", i=n, u=2),
-                in_=bank[:, 0:n, :, :].rearrange("p i u c -> p i c u"),
+        x_by_tile = x_tok[:].rearrange("p (i d) -> p d i", d=D)
+        x_words = x_pairs[:].rearrange("p d i e -> p (d i e)").bitcast(F32)
+        x1_words = x1_four[:].rearrange("p q c -> p (q c)").bitcast(F32)
+
+        def pair_x(first, last):
+            nc.vector.tensor_copy(
+                out=x_pairs[:, first:last, :, :],
+                in_=x_by_tile[:, first:last, :].unsqueeze(3).to_broadcast([P, last - first, FIELDS, 2]),
             )
+
+        def widen_x(n):
+            fields = slice(16 * n, 16 * n + 16)
+            nc.vector.tensor_copy(out=x_wide[:, fields, :], in_=x_words[:, fields].unsqueeze(2).to_broadcast([P, 16, 32]))
+
+        nc.vector.tensor_copy(
+            out=x1_four[:, 0, :].rearrange("p (j d e) -> p j d e", d=TILES, e=2),
+            in_=x1_tok[:].rearrange("p (j e d) -> p j d e", e=2, d=D)[:, :, 0:TILES, :],
+        )
+        nc.scalar.copy(out=x1_four[:, 1, :], in_=x1_four[:, 0, :])
+        nc.vector.tensor_copy(out=x1_four[:, 2:4, :], in_=x1_four[:, 0:1, :].to_broadcast([P, 2, 1024]))
+        pair_x(0, 1)
+        widen_x(0)
+        pair_x(1, TILES)
+        for n in range(1, 4):
+            widen_x(n)
+
+        def turn_x1(first, count):
+            bank = psum.tile([P, 2, 2, P], F32, name="bank", bufs=3)
+            for i in range(count):
+                for u in range(2):
+                    nc.tensor.transpose(bank[:, i, u, :], x1_words[:, 8 * u + first + i : 2048 : 16], ident[:])
+            words = x1_by_k[:, first : first + count, :].rearrange("p i c -> p (i c)").bitcast(F32)
+            nc.scalar.copy(
+                out=words.rearrange("p (i c u) -> p i c u", i=count, u=2),
+                in_=bank[:, 0:count, :, :].rearrange("p i u c -> p i c u"),
+            )
+
+        x_banks = {}
+
+        def turn_x(s):
+            bank = psum.tile([P, 4, P], F32, name="x_bank" if s < 2 else "acc1", bufs=2)
+            rows = x_wide[:].rearrange("p i r -> p (i r)")
+            for g in range(4):
+                lo = 512 * s + 128 * g
+                nc.tensor.transpose(bank[:, g, :], rows[:, lo : lo + 128], ident[:])
+            x_banks[s] = bank
+
         turn_x1(0, 1)
         turn_x(0)
-        first = psum.tile([P, 4, P], F32, name="bank", bufs=3)
-        for h in range(4):
-            nc.tensor.transpose(first[:, h, :], x_words[:, 128 * h : 128 * h + 128], ident[:])
-        for h0, h1 in ((0, 1), (1, 4)):
-            nc.scalar.copy(out=xt[:, h0:h1, :, :], in_=first[:, h0:h1, :].unsqueeze(3).to_broadcast([P, h1 - h0, P, 2]))
-        x_view = out.rearrange("(g q) n -> q g n", q=4)
-        xb = {}
-        def spread(t):
-            d = 64 * (t % 2)
-            nc.sync.dma_start(out=out, in_=xt[d : d + 64, t // 2, :, :].rearrange("p c e -> p (c e)"))
-            for h in range(2):
-                if not (t == 1 and h == 1):
-                    spread_half(t, h)
-        def spread_half(t, h):
-            b = work.tile([P, 8, 256], F32, name="xb", bufs=6)
-            for q in range(4):
-                nc.sync.dma_start(out=b[32 * q : 32 * q + 32, :, :], in_=x_view[q, 8 * h : 8 * h + 8, :].partition_broadcast(32))
-            xb[t, h] = b
-        spread(1)
-        load_w1(1)
-        spread_half(1, 1)
-        for k in range(2, 4):
-            load_w1(k)
+
+        bank = psum.tile([P, 4, P], F32, name="bank", bufs=3)
+        for half in range(4):
+            nc.tensor.transpose(bank[:, half, :], x_words[:, 128 * half : 128 * half + 128], ident[:])
+        for first, last in ((0, 1), (1, 4)):
+            nc.scalar.copy(out=x_turned[:, first:last, :], in_=bank[:, first:last, :])
+
+        parked = out.rearrange("b (h n) -> (b h) n", h=2)
+        parked_rows = parked.rearrange("(d g q) n -> d q g n", d=2, q=4)
+        x_by_k = {}
+
+        def park_x(pair):
+            nc.sync.dma_start(out=parked, in_=x_turned[:, pair, :])
+
+        def load_x(t, queue, quadrants):
+            for half in range(2):
+                if (t, half) not in x_by_k:
+                    x_by_k[t, half] = work.tile([P, 8, P], F32, name="x_by_k", bufs=8)
+                for q in quadrants:
+                    queue.dma_start(
+                        out=x_by_k[t, half][32 * q : 32 * q + 32, :, :],
+                        in_=parked_rows[t % 2, q, 8 * half : 8 * half + 8, :].partition_broadcast(32),
+                    )
+
+        park_x(0)
+        load_x(1, nc.sync, (0, 1))
+        for n in range(1, 4):
+            load_w1(n)
         load_w2(1)
         nc.sync.dma_start(out=b1_row[:], in_=b1.partition_broadcast(P))
         nc.sync.dma_start(out=b2_row[:], in_=b2.partition_broadcast(P))
-        spread(2)
 
-        z1_tiles = {}
-        def outer1(s):
-            z1 = work.tile([P, 2048], BF16, name="z1", align_bytes=64, bufs=3)
-            g = 4 * (s % 4)
-            if s >= 4:
-                nc.vector.tensor_tensor(
-                    out=z1[:].rearrange("p (g c) -> p g c", g=4),
-                    in0=xb[s // 4, s % 4 // 2][:, g % 8 : g % 8 + 4, :].rearrange("p g c -> p (g c)").bitcast(BF16).rearrange("p (g c) -> p g c", g=4),
-                    in1=xk[:, s // 4, :].unsqueeze(1).to_broadcast([P, 4, 512]),
-                    op=MULT,
-                )
-                z1_tiles[s] = z1
-                return
-            words = x_bank.pop(s)[:]
-            nc.vector.tensor_tensor(
-                out=z1[:].rearrange("p (g c a e) -> p g c a e", g=4, a=2, e=2),
-                in0=words.rearrange("p g c -> p (g c)").bitcast(BF16).rearrange("p (g c e) -> p g c e", g=4, e=2).unsqueeze(3).to_broadcast([P, 4, P, 2, 2]),
-                in1=xk[:, s // 4, :].rearrange("p (c a e) -> p c a e", a=2, e=2).unsqueeze(1).to_broadcast([P, 4, P, 2, 2]),
-                op=MULT,
+        def group(raw, engine):
+            grouped = work.tile([P, 4, P, 4], BF16, name="w_grouped", align_bytes=64, bufs=5)
+            source = raw[:].rearrange("p g t n -> p g n t")
+            if engine == "vector":
+                nc.vector.tensor_copy(out=grouped[:], in_=source)
+            elif engine == "scalar":
+                nc.scalar.copy(out=grouped[:], in_=source)
+            else:
+                for g in range(0, 4, 2):
+                    bank = psum.tile([P, 2, 512], BF16, name="bank", bufs=3)
+                    for i in range(2):
+                        nc.tensor.matmul(bank[:, i, :], lhsT=ident16[:], rhs=source[:, g + i, :, :], start=True, stop=True)
+                    nc.scalar.copy(
+                        out=grouped[:, g : g + 2, :, :].rearrange("p g n t -> p (g n t)"),
+                        in_=bank[:].rearrange("p i c -> p (i c)"),
+                    )
+            return grouped
+
+        def quantize_weight(grouped, n, codes, scales):
+            cols = slice(512 * n, 512 * n + 512)
+            nc.vector.quantize_mx(
+                out=codes[:, cols].bitcast(FP8X4),
+                scales=scales[:, cols],
+                in_=grouped[:].rearrange("p g n t -> p (g n t)"),
             )
-            z1_tiles[s] = z1
-        codes1 = {}
-        def quantize1(s):
-            c = work.tile([P, 512], U32, name="z1_codes", align_bytes=64, bufs=7)
-            sc = work.tile([P, 512], U8, name="z1_scales", align_bytes=64, bufs=7)
-            nc.vector.quantize_mx(out=c[:].bitcast(FP8X4), scales=sc[:], in_=z1_tiles.pop(s)[:])
-            codes1[s] = (c, sc)
 
-        def product(acc, codes, s, w_codes, w_scales, first, last):
-            c, sc = codes
+        def widen_w2(n):
+            wide = work.tile([P, 4, 4, P], BF16, name="w2_wide", bufs=3)
+            for g in range(4):
+                for t in range(4):
+                    k = 4 * (4 * n + g) + t
+                    nc.scalar.activation(
+                        out=wide[:, g, t, :],
+                        in_=w2_codes8[:, 4 * n + g, 128 * t : 128 * t + 128].bitcast(FP8),
+                        func=COPY,
+                        scale=w2_scales32[:, k : k + 1],
+                    )
+            return wide
+
+        def quantize(values, name, bufs):
+            codes = work.tile([P, 512], U32, name=name + "_codes", align_bytes=64, bufs=bufs)
+            scales = work.tile([P, 512], U8, name=name + "_scales", align_bytes=64, bufs=bufs)
+            nc.vector.quantize_mx(out=codes[:].bitcast(FP8X4), scales=scales[:], in_=values[:])
+            return codes, scales
+
+        def multiply(acc, operand, s, w_codes, w_scales, start, stop):
+            codes, scales = operand
             for g in range(4):
                 cols = slice(128 * g, 128 * g + 128)
-                wcols = slice(128 * (4 * (s % 4) + g), 128 * (4 * (s % 4) + g) + 128)
+                w_lo = 128 * (4 * (s % 4) + g)
+                w_cols = slice(w_lo, w_lo + 128)
                 nc.tensor.matmul_mx(
-                    out=acc, lhsT=c[:, cols].bitcast(FP8X4), lhsT_scale=sc[:, cols],
-                    rhs=w_codes[:, wcols].bitcast(FP8X4), rhs_scale=w_scales[:, wcols],
-                    start=(first and g == 0), stop=(last and g == 3),
-                )
-        acc1 = {}
-        def matmul1(s):
-            if s % 4 == 0:
-                acc1[s // 4] = psum.tile([P, P], F32, name="acc1", bufs=2)
-            product(acc1[s // 4][:], codes1.pop(s), s, w1_codes, w1_scales, s % 4 == 0, s % 4 == 3)
-        acc2 = psum.tile([P, P], F32, name="acc2")
-        codes2 = {}
-        def matmul2(m):
-            c, sc = codes2[m]
-            product(acc2[:], codes2.pop(m), m, w2_codes, w2_scales, m == 0, m == STEPS - 1)
-            for i in range(WARM):
-                dummy = psum.tile([P, 512], F32, name="dummy", bufs=1)
-                nc.tensor.matmul_mx(
-                    out=dummy[:], lhsT=c[:, 0:128].bitcast(FP8X4), lhsT_scale=sc[:, 0:128],
-                    rhs=w2_codes[:, 0:512].bitcast(FP8X4), rhs_scale=w2_scales[:, 0:512], start=True, stop=True,
+                    out=acc,
+                    lhsT=codes[:, cols].bitcast(FP8X4),
+                    lhsT_scale=scales[:, cols],
+                    rhs=w_codes[:, w_cols].bitcast(FP8X4),
+                    rhs_scale=w_scales[:, w_cols],
+                    start=(start and g == 0),
+                    stop=(stop and g == 3),
                 )
 
-        def leave1(t):
+        def keep_clock(operand):
+            codes, scales = operand
+            spare = psum.tile([P, 512], F32, name="x_bank", bufs=2)
+            nc.tensor.matmul_mx(
+                out=spare[:],
+                lhsT=codes[:, 0:128].bitcast(FP8X4),
+                lhsT_scale=scales[:, 0:128],
+                rhs=w2_codes[:, 0:512].bitcast(FP8X4),
+                rhs_scale=w2_scales[:, 0:512],
+                start=True,
+                stop=True,
+            )
+
+        def make_z1(s):
+            if s < 4:
+                words = x_banks.pop(s)[:]
+            else:
+                lo = 4 * (s % 2)
+                words = x_by_k[s // 4, s % 4 // 2][:, lo : lo + 4, :]
+            pairs = words.rearrange("p g c -> p (g c)").bitcast(BF16).rearrange("p (g c e) -> p g c e", g=4, e=2)
+            maps = x1_by_k[:, s // 4, :].rearrange("p (c u e) -> p c u e", u=2, e=2)
+            z1 = work.tile([P, CHUNK], BF16, name="z1", align_bytes=64, bufs=3)
+            nc.vector.tensor_tensor(
+                out=z1[:].rearrange("p (g c u e) -> p g c u e", g=4, u=2, e=2),
+                in0=pairs.unsqueeze(3).to_broadcast([P, 4, P, 2, 2]),
+                in1=maps.unsqueeze(1).to_broadcast([P, 4, P, 2, 2]),
+                op=MULT,
+            )
+            return z1
+
+        def leave_layer1(t, acc):
             nc.vector.tensor_tensor(
                 out=o1[:, t, :].rearrange("p (u m e) -> p u m e", u=2, e=2),
-                in0=acc1.pop(t)[:].rearrange("p (m u e) -> p u m e", u=2, e=2),
+                in0=acc[:].rearrange("p (m u e) -> p u m e", u=2, e=2),
                 in1=b1_row[:].rearrange("p (m u e) -> p u m e", u=2, e=2),
                 op=ADD,
             )
-        def sum1(t):
             if t > 0:
-                nc.gpsimd.tensor_tensor(out=fin[:, 0:128], in0=(o1[:, 0, :] if t == 1 else fin[:, 0:128]), in1=o1[:, t, :], op=ADD)
+                before = o1[:, 0, :] if t == 1 else sums[:, 0:P]
+                nc.gpsimd.tensor_tensor(out=sums[:, 0:P], in0=before, in1=o1[:, t, :], op=ADD)
 
-        def finish(h):
-            cols = slice(128 * h, 128 * h + 128)
-            if h == 1:
-                nc.vector.scalar_tensor_tensor(out=fin[:, cols], in0=b2_row[:], scalar=8.0, in1=acc2[:], op0=MULT, op1=ADD)
-            total = psum.tile([P, P], F32, name="bank", bufs=3)
-            nc.tensor.matmul(total[:], lhsT=sel[:], rhs=fin[:, cols], start=True, stop=True)
-            if h == 0:
-                nc.scalar.copy(
-                    out=res[:, cols].rearrange("p (m u e) -> p m u e", u=2, e=2),
-                    in_=total[:].rearrange("p (u m e) -> p m u e", u=2, e=2),
-                )
-            else:
-                nc.vector.tensor_copy(out=res[:, cols], in_=total[:])
-            nc.sync.dma_start(out=out[:, cols], in_=res[0:64, cols])
-
-        z2_tm = {}
-        def outer2(m, order):
-            z = work.tile([P, 2, 16, 64], BF16, name="z2_tm", bufs=3)
-            src = o1[:, m // 4, :].rearrange("p (u c) -> p u c", u=2)
+        def make_z2(m):
+            z2 = work.tile([P, 2, 16, 64], BF16, name="z2", bufs=3)
+            source = o1[:, m // 4, :].rearrange("p (u c) -> p u c", u=2)
+            share = vector_products(m)
             for r in range(16):
                 i = 16 * (m % 4) + r
-                scale = xs[:, m // 4, i : i + 1]
-                if order[r] == "S":
-                    nc.scalar.activation(out=z[:, :, r, :], in_=src, func=COPY, scale=scale)
+                scale = x_scale[:, m // 4, i : i + 1]
+                if (r + 1) * share // 16 > r * share // 16:
+                    nc.vector.tensor_scalar(out=z2[:, :, r, :], in0=source, scalar1=scale, scalar2=None, op0=MULT)
                 else:
-                    nc.vector.tensor_scalar(out=z[:, :, r, :], in0=src, scalar1=scale, scalar2=None, op0=MULT)
-            z2_tm[m] = z
-        z2_banks = {}
-        def turn2(m):
-            words = z2_tm.pop(m)[:].rearrange("p u r c -> p (u r c)").bitcast(F32)
-            for h in range(2):
+                    nc.scalar.activation(out=z2[:, :, r, :], in_=source, func=COPY, scale=scale)
+            return z2
+
+        def turn_z2(z2):
+            words = z2[:].rearrange("p u r c -> p (u r c)").bitcast(F32)
+            banks = []
+            for half in range(2):
                 bank = psum.tile([P, 2, 2, P], F32, name="bank", bufs=3)
                 for g in range(2):
                     for u in range(2):
-                        lo = 512 * u + 128 * (2 * h + g)
+                        lo = 512 * u + 128 * (2 * half + g)
                         nc.tensor.transpose(bank[:, g, u, :], words[:, lo : lo + 128], ident[:])
-                z2_banks[m, h] = bank
-        z2_km = {}
-        def leave2(m, engines):
-            z = work.tile([P, 2048], BF16, name="z2_km", align_bytes=64, bufs=3)
-            words = z[:].bitcast(F32).rearrange("p (g c u) -> p g c u", g=4, u=2)
-            for h in range(2):
-                src = z2_banks.pop((m, h))[:].rearrange("p g u c -> p g c u")
-                if engines[h] == "S":
-                    nc.scalar.copy(out=words[:, 2 * h : 2 * h + 2, :, :], in_=src)
-                else:
-                    nc.vector.tensor_copy(out=words[:, 2 * h : 2 * h + 2, :, :], in_=src)
-            z2_km[m] = z
-        def quantize2(m):
-            c = work.tile([P, 512], U32, name="z2_codes", align_bytes=64, bufs=3)
-            sc = work.tile([P, 512], U8, name="z2_scales", align_bytes=64, bufs=3)
-            nc.vector.quantize_mx(out=c[:].bitcast(FP8X4), scales=sc[:], in_=z2_km.pop(m)[:])
-            codes2[m] = (c, sc)
+                banks.append(bank)
+            return banks
 
-        grouped = {}
-        def interleave(key, raw, engine):
-            g = work.tile([P, 4, P, 4], BF16, name="w_grouped", align_bytes=64, bufs=5)
-            src = raw[:].rearrange("p g t n -> p g n t")
-            if engine == "V":
-                nc.vector.tensor_copy(out=g[:], in_=src)
+        def leave_banks(banks, m):
+            z2_by_k = work.tile([P, CHUNK], BF16, name="z2_by_k", align_bytes=64, bufs=3)
+            words = z2_by_k[:].bitcast(F32).rearrange("p (g c u) -> p g c u", g=4, u=2)
+            for half in range(2):
+                target = words[:, 2 * half : 2 * half + 2, :, :]
+                source = banks[half][:].rearrange("p g u c -> p g c u")
+                if m == CHUNKS - 1 and half == 0:
+                    nc.vector.tensor_copy(out=target, in_=source)
+                else:
+                    nc.scalar.copy(out=target, in_=source)
+            return z2_by_k
+
+        def finish(layer):
+            cols = slice(P * layer, P * layer + P)
+            total = psum.tile([P, P], F32, name="bank", bufs=3)
+            nc.tensor.matmul(total[:], lhsT=fold[:], rhs=sums[:, cols], start=True, stop=True)
+            if layer == 0:
+                nc.scalar.copy(
+                    out=result[:, cols].rearrange("p (m u e) -> p m u e", u=2, e=2),
+                    in_=total[:].rearrange("p (u m e) -> p m u e", u=2, e=2),
+                )
             else:
-                for h in range(2):
-                    bank = psum.tile([P, 2, 512], BF16, name="bank", bufs=3)
-                    for i in range(2):
-                        nc.tensor.matmul(bank[:, i, :], lhsT=ident16[:], rhs=src[:, 2 * h + i, :, :], start=True, stop=True)
-                    nc.scalar.copy(out=g[:, 2 * h : 2 * h + 2, :, :].rearrange("p g n t -> p (g n t)"), in_=bank[:].rearrange("p i c -> p (i c)"))
-            grouped[key] = g
-        def quantize_w(key, k, codes, scales):
-            cols = slice(512 * k, 512 * k + 512)
-            nc.vector.quantize_mx(out=codes[:, cols].bitcast(FP8X4), scales=scales[:, cols], in_=grouped.pop(key)[:].rearrange("p g n t -> p (g n t)"))
-        w2_wide = {}
-        def widen_w2(k):
-            w = work.tile([P, 4, 4, P], BF16, name="w2_wide", bufs=3)
-            for g in range(4):
-                for t in range(4):
-                    gg = 4 * k + g
-                    nc.scalar.activation(
-                        out=w[:, g, t, :], in_=w2_raw[:, gg, 128 * t : 128 * t + 128].bitcast(FP8),
-                        func=COPY, scale=w2_sc[:, 4 * gg + t : 4 * gg + t + 1],
-                    )
-            w2_wide[k] = w
+                nc.vector.tensor_copy(out=result[:, cols], in_=total[:])
+            nc.sync.dma_start(out=out[:, cols], in_=result[0:64, cols])
 
         turn_x1(1, 1)
-        for k in range(1, 4):
-            turn_x(k)
-        for s in range(-1, STEPS + LAG + 4):
-            for h in range(1, 4):
-                if X1[h] == s:
-                    turn_x1(2 * h, 2)
+        for s in range(1, 4):
+            turn_x(s)
+
+        acc1 = {}
+        acc2 = psum.tile([P, P], F32, name="acc2")
+        z1, z1_mx = {}, {}
+        z2, z2_banks, z2_by_k, z2_mx = {}, {}, {}, {}
+        w2_wide, w1_grouped, w2_grouped = {}, {}, {}
+
+        for s in range(-1, CHUNKS + Z2_LAG + 4):
+            m = s - Z2_LAG
+
+            for pair in range(3):
+                if X1_TURN_STEP[pair] == s:
+                    turn_x1(2 * pair + 2, 2)
             if s == 2:
-                nc.scalar.copy(out=xs[:], in_=x_dm[:, 0:TILES, :])
-            if not WFIRST:
-                for k in range(4):
-                    if W1I[k] == s:
-                        interleave(("w1", k), w1_raw[k], W1_ENGINE[k])
-            if s in SPREAD:
-                spread(SPREAD[s])
-            for k in range(4):
-                if W2W[k] == s:
-                    widen_w2(k)
-            if WFIRST:
-                for k in range(4):
-                    if W1I[k] == s:
-                        interleave(("w1", k), w1_raw[k], W1_ENGINE[k])
-            if s < 0:
-                continue
-            m = s - LAG
-            if 0 <= m - 1 < STEPS:
-                turn2(m - 1)
-            if 0 <= s - ML < STEPS:
-                matmul1(s - ML)
-            if 0 <= m - 3 < STEPS:
-                matmul2(m - 3)
-            if s < STEPS:
-                outer1(s)
-            for k in range(4):
-                if W2I[k] == s:
-                    interleave(("w2", k), w2_wide.pop(k), W2_ENGINE[k])
-            if 0 <= m - 2 < STEPS:
-                quantize2(m - 2)
-            for k in range(4):
-                if W1Q[k] == s:
-                    quantize_w(("w1", k), k, w1_codes, w1_scales)
-                if W2Q[k] == s:
-                    quantize_w(("w2", k), k, w2_codes, w2_scales)
-            if 0 <= m < STEPS:
-                outer2(m, ORDERS[m])
-            if 0 <= m - 1 < STEPS:
-                leave2(m - 1, EVAC[m - 1])
-            if s < STEPS:
-                quantize1(s)
-            f = s - ML - 3
-            if f >= 0 and f % 4 == 0 and f < STEPS:
-                leave1(f // 4)
-                sum1(f // 4)
-            if s == STEPS + ML + 3:
+                nc.scalar.copy(out=x_scale[:], in_=x_by_tile[:, 0:TILES, :])
+            for pair in range(3):
+                if X_PARK_STEP[pair] == s:
+                    park_x(pair + 1)
+                    for t in (2 * pair + 2, 2 * pair + 3):
+                        load_x(t, nc.sync, range(4))
+            for n in range(4):
+                if W2_WIDEN_STEP[n] == s:
+                    w2_wide[n] = widen_w2(n)
+            if s == 0:
+                load_x(1, nc.scalar, (2, 3))
+            for n in range(4):
+                if W1_GROUP_STEP[n] == s:
+                    w1_grouped[n] = group(w1_raw[n], W1_GROUP_ENGINE[n])
+
+            if 0 <= m - 1 < CHUNKS:
+                z2_banks[m - 1] = turn_z2(z2.pop(m - 1))
+            done = s - MATMUL1_LAG
+            if 0 <= done < CHUNKS:
+                if done % 4 == 0:
+                    acc1[done // 4] = psum.tile([P, P], F32, name="acc1", bufs=2)
+                multiply(acc1[done // 4][:], z1_mx.pop(done), done, w1_codes, w1_scales, done % 4 == 0, done % 4 == 3)
+            if 0 <= m - 3 < CHUNKS:
+                multiply(acc2[:], z2_mx[m - 3], m - 3, w2_codes, w2_scales, m == 3, m - 3 == CHUNKS - 1)
+                keep_clock(z2_mx.pop(m - 3))
+
+            if 0 <= s < CHUNKS:
+                z1[s] = make_z1(s)
+            for n in range(4):
+                if W2_GROUP_STEP[n] == s:
+                    w2_grouped[n] = group(w2_wide.pop(n), W2_GROUP_ENGINE[n])
+            if 0 <= m - 2 < CHUNKS:
+                z2_mx[m - 2] = quantize(z2_by_k.pop(m - 2), "z2", 3)
+            for n in range(4):
+                if W1_QUANTIZE_STEP[n] == s:
+                    quantize_weight(w1_grouped.pop(n), n, w1_codes, w1_scales)
+                if W2_QUANTIZE_STEP[n] == s:
+                    quantize_weight(w2_grouped.pop(n), n, w2_codes, w2_scales)
+            if 0 <= m < CHUNKS:
+                z2[m] = make_z2(m)
+            if 0 <= m - 1 < CHUNKS:
+                z2_by_k[m - 1] = leave_banks(z2_banks.pop(m - 1), m - 1)
+            if 0 <= s < CHUNKS:
+                z1_mx[s] = quantize(z1.pop(s), "z1", 8)
+            if 0 <= done < CHUNKS and done % 4 == 3:
+                leave_layer1(done // 4, acc1.pop(done // 4))
+            if m == CHUNKS - 2:
                 finish(0)
 
+        nc.vector.scalar_tensor_tensor(
+            out=sums[:, P : 2 * P], in0=b2_row[:], scalar=float(TILES), in1=acc2[:], op0=MULT, op1=ADD
+        )
         finish(1)

from contextlib import ExitStack

import concourse.mybir as mybir
from concourse.masks import make_identity

F32 = mybir.dt.float32
BF16 = mybir.dt.bfloat16
U32 = mybir.dt.uint32
U8 = mybir.dt.uint8
FP8 = mybir.dt.float8_e4m3fn
FP8X4 = mybir.dt.float8_e4m3fn_x4
MULT = mybir.AluOpType.mult
ADD = mybir.AluOpType.add
COPY = mybir.ActivationFunctionType.Copy

P = 128
D = 16
FIELDS = 64
TILES = 8
CHUNK = 2048
CHUNKS = TILES * 4

FLOPS = 2 * 2 * 1024 * 8192 * 128

MATMUL1_LAG = 5
Z2_LAG = 10

W1_GROUP_STEP = (0, 1, 1, 5)
W1_GROUP_ENGINE = ("vector", "scalar", "scalar", "tensor")
W1_QUANTIZE_STEP = (3, 5, 6, 7)
W2_WIDEN_STEP = (1, 1, 3, 6)
W2_GROUP_STEP = (2, 4, 7, 8)
W2_GROUP_ENGINE = ("vector", "vector", "tensor", "tensor")
W2_QUANTIZE_STEP = (8, 9, 9, 13)
X1_TURN_STEP = (-1, 2, 7)
X_PARK_STEP = (1, 9, 17)


def vector_products(m):
    if m < 8:
        return 6
    return 5 if m + Z2_LAG < CHUNKS else 12


def tile_cin_pa_kernel(tc, x, x1, w1, b1, w2_bytes, w2_scale, b2, out):
    nc = tc.nc
    with ExitStack() as ctx:
        keep = ctx.enter_context(tc.tile_pool(name="keep", bufs=1))
        work = ctx.enter_context(tc.tile_pool(name="work", bufs=3))
        psum = ctx.enter_context(tc.psum_pool(name="psum", bufs=1))
        ctx.enter_context(tc.manual_schedule())

        x_tok = keep.tile([P, FIELDS * D], BF16, name="x_tok")
        x1_tok = keep.tile([P, P * D], BF16, name="x1_tok")
        x_pairs = keep.tile([P, TILES, FIELDS, 2], BF16, name="x_pairs")
        x_wide = keep.tile([P, FIELDS, 32], F32, name="x_wide")
        x_turned = keep.tile([P, 4, P], F32, name="x_turned")
        x_scale = keep.tile([P, TILES, FIELDS], F32, name="x_scale")
        x1_four = keep.tile([P, 4, 1024], BF16, name="x1_four")
        x1_by_k = keep.tile([P, TILES, 512], BF16, name="x1_by_k")
        ident = keep.tile([P, P], F32, name="ident")
        ident16 = keep.tile([P, P], BF16, name="ident16")
        fold = keep.tile([P, P], F32, name="fold")
        b1_row = keep.tile([P, P], BF16, name="b1_row")
        b2_row = keep.tile([P, P], BF16, name="b2_row")
        w2_codes8 = keep.tile([P, 16, 512], U8, name="w2_codes8")
        w2_scales32 = keep.tile([P, 64], F32, name="w2_scales32")
        w1_codes = keep.tile([P, 16 * P], U32, name="w1_codes", align_bytes=64)
        w1_scales = keep.tile([P, 16 * P], U8, name="w1_scales", align_bytes=64)
        w2_codes = keep.tile([P, 16 * P], U32, name="w2_codes", align_bytes=64)
        w2_scales = keep.tile([P, 16 * P], U8, name="w2_scales", align_bytes=64)
        o1 = keep.tile([P, TILES, P], F32, name="o1")
        sums = keep.tile([P, 2 * P], F32, name="sums")
        result = keep.tile([P, 2 * P], F32, name="result")

        x_rows = x.rearrange("b i d -> b (i d)")
        x1_rows = x1.rearrange("b j d -> b (j d)")
        nc.sync.dma_start(out=x1_tok[0:64, :], in_=x1_rows)
        nc.scalar.dma_start(out=x1_tok[64:128, 0 : P * D - 8], in_=x1_rows[:, 8 : P * D])
        nc.sync.dma_start(out=x_tok[0:64, :], in_=x_rows)
        nc.scalar.dma_start(out=x_tok[64:128, 0 : FIELDS * D - 8], in_=x_rows[:, 8 : FIELDS * D])

        w1_view = w1.rearrange("(g p t) n -> p g (t n)", p=P, t=4)
        w2_view = w2_bytes.rearrange("(g p t) n -> p g (t n)", p=P, t=4)
        w1_raw = []

        def load_w1(n):
            raw = work.tile([P, 4, 4, P], BF16, name="w1_raw", bufs=4)
            nc.sync.dma_start(out=raw[:].rearrange("p g t n -> p g (t n)"), in_=w1_view[:, 4 * n : 4 * n + 4, :])
            w1_raw.append(raw)

        def load_w2(half):
            passes = slice(8 * half, 8 * half + 8)
            nc.sync.dma_start(out=w2_codes8[:, passes, :], in_=w2_view[:, passes, :])

        load_w1(0)
        nc.sync.dma_start(
            out=w2_scales32[:].rearrange("p (g t) -> p g t", t=4),
            in_=w2_scale.rearrange("(g p t) o -> p g (t o)", p=P, t=4),
        )
        load_w2(0)

        make_identity(nc, ident[:])
        nc.gpsimd.memset(fold[:], 0.0)
        nc.gpsimd.tensor_tensor(out=fold[:, 0:64], in0=ident[:, 0:64], in1=ident[:, 64:128], op=ADD)
        nc.gpsimd.tensor_copy(out=ident16[:], in_=ident[:])

        x_by_tile = x_tok[:].rearrange("p (i d) -> p d i", d=D)
        x_words = x_pairs[:].rearrange("p d i e -> p (d i e)").bitcast(F32)
        x1_words = x1_four[:].rearrange("p q c -> p (q c)").bitcast(F32)

        def pair_x(first, last):
            nc.vector.tensor_copy(
                out=x_pairs[:, first:last, :, :],
                in_=x_by_tile[:, first:last, :].unsqueeze(3).to_broadcast([P, last - first, FIELDS, 2]),
            )

        def widen_x(n):
            fields = slice(16 * n, 16 * n + 16)
            nc.vector.tensor_copy(out=x_wide[:, fields, :], in_=x_words[:, fields].unsqueeze(2).to_broadcast([P, 16, 32]))

        nc.vector.tensor_copy(
            out=x1_four[:, 0, :].rearrange("p (j d e) -> p j d e", d=TILES, e=2),
            in_=x1_tok[:].rearrange("p (j e d) -> p j d e", e=2, d=D)[:, :, 0:TILES, :],
        )
        nc.scalar.copy(out=x1_four[:, 1, :], in_=x1_four[:, 0, :])
        nc.vector.tensor_copy(out=x1_four[:, 2:4, :], in_=x1_four[:, 0:1, :].to_broadcast([P, 2, 1024]))
        pair_x(0, 1)
        widen_x(0)
        pair_x(1, TILES)
        for n in range(1, 4):
            widen_x(n)

        def turn_x1(first, count):
            bank = psum.tile([P, 2, 2, P], F32, name="bank", bufs=3)
            for i in range(count):
                for u in range(2):
                    nc.tensor.transpose(bank[:, i, u, :], x1_words[:, 8 * u + first + i : 2048 : 16], ident[:])
            words = x1_by_k[:, first : first + count, :].rearrange("p i c -> p (i c)").bitcast(F32)
            nc.scalar.copy(
                out=words.rearrange("p (i c u) -> p i c u", i=count, u=2),
                in_=bank[:, 0:count, :, :].rearrange("p i u c -> p i c u"),
            )

        x_banks = {}

        def turn_x(s):
            bank = psum.tile([P, 4, P], F32, name="x_bank" if s < 2 else "acc1", bufs=2)
            rows = x_wide[:].rearrange("p i r -> p (i r)")
            for g in range(4):
                lo = 512 * s + 128 * g
                nc.tensor.transpose(bank[:, g, :], rows[:, lo : lo + 128], ident[:])
            x_banks[s] = bank

        turn_x1(0, 1)
        turn_x(0)

        bank = psum.tile([P, 4, P], F32, name="bank", bufs=3)
        for half in range(4):
            nc.tensor.transpose(bank[:, half, :], x_words[:, 128 * half : 128 * half + 128], ident[:])
        for first, last in ((0, 1), (1, 4)):
            nc.scalar.copy(out=x_turned[:, first:last, :], in_=bank[:, first:last, :])

        parked = out.rearrange("b (h n) -> (b h) n", h=2)
        parked_rows = parked.rearrange("(d g q) n -> d q g n", d=2, q=4)
        x_by_k = {}

        def park_x(pair):
            nc.sync.dma_start(out=parked, in_=x_turned[:, pair, :])

        def load_x(t, queue, quadrants):
            for half in range(2):
                if (t, half) not in x_by_k:
                    x_by_k[t, half] = work.tile([P, 8, P], F32, name="x_by_k", bufs=8)
                for q in quadrants:
                    queue.dma_start(
                        out=x_by_k[t, half][32 * q : 32 * q + 32, :, :],
                        in_=parked_rows[t % 2, q, 8 * half : 8 * half + 8, :].partition_broadcast(32),
                    )

        park_x(0)
        load_x(1, nc.sync, (0, 1))
        for n in range(1, 4):
            load_w1(n)
        load_w2(1)
        nc.sync.dma_start(out=b1_row[:], in_=b1.partition_broadcast(P))
        nc.sync.dma_start(out=b2_row[:], in_=b2.partition_broadcast(P))

        def group(raw, engine):
            grouped = work.tile([P, 4, P, 4], BF16, name="w_grouped", align_bytes=64, bufs=5)
            source = raw[:].rearrange("p g t n -> p g n t")
            if engine == "vector":
                nc.vector.tensor_copy(out=grouped[:], in_=source)
            elif engine == "scalar":
                nc.scalar.copy(out=grouped[:], in_=source)
            else:
                for g in range(0, 4, 2):
                    bank = psum.tile([P, 2, 512], BF16, name="bank", bufs=3)
                    for i in range(2):
                        nc.tensor.matmul(bank[:, i, :], lhsT=ident16[:], rhs=source[:, g + i, :, :], start=True, stop=True)
                    nc.scalar.copy(
                        out=grouped[:, g : g + 2, :, :].rearrange("p g n t -> p (g n t)"),
                        in_=bank[:].rearrange("p i c -> p (i c)"),
                    )
            return grouped

        def quantize_weight(grouped, n, codes, scales):
            cols = slice(512 * n, 512 * n + 512)
            nc.vector.quantize_mx(
                out=codes[:, cols].bitcast(FP8X4),
                scales=scales[:, cols],
                in_=grouped[:].rearrange("p g n t -> p (g n t)"),
            )

        def widen_w2(n):
            wide = work.tile([P, 4, 4, P], BF16, name="w2_wide", bufs=3)
            for g in range(4):
                for t in range(4):
                    k = 4 * (4 * n + g) + t
                    nc.scalar.activation(
                        out=wide[:, g, t, :],
                        in_=w2_codes8[:, 4 * n + g, 128 * t : 128 * t + 128].bitcast(FP8),
                        func=COPY,
                        scale=w2_scales32[:, k : k + 1],
                    )
            return wide

        def quantize(values, name, bufs):
            codes = work.tile([P, 512], U32, name=name + "_codes", align_bytes=64, bufs=bufs)
            scales = work.tile([P, 512], U8, name=name + "_scales", align_bytes=64, bufs=bufs)
            nc.vector.quantize_mx(out=codes[:].bitcast(FP8X4), scales=scales[:], in_=values[:])
            return codes, scales

        def multiply(acc, operand, s, w_codes, w_scales, start, stop):
            codes, scales = operand
            for g in range(4):
                cols = slice(128 * g, 128 * g + 128)
                w_lo = 128 * (4 * (s % 4) + g)
                w_cols = slice(w_lo, w_lo + 128)
                nc.tensor.matmul_mx(
                    out=acc,
                    lhsT=codes[:, cols].bitcast(FP8X4),
                    lhsT_scale=scales[:, cols],
                    rhs=w_codes[:, w_cols].bitcast(FP8X4),
                    rhs_scale=w_scales[:, w_cols],
                    start=(start and g == 0),
                    stop=(stop and g == 3),
                )

        def keep_clock(operand):
            codes, scales = operand
            spare = psum.tile([P, 512], F32, name="x_bank", bufs=2)
            nc.tensor.matmul_mx(
                out=spare[:],
                lhsT=codes[:, 0:128].bitcast(FP8X4),
                lhsT_scale=scales[:, 0:128],
                rhs=w2_codes[:, 0:512].bitcast(FP8X4),
                rhs_scale=w2_scales[:, 0:512],
                start=True,
                stop=True,
            )

        def make_z1(s):
            if s < 4:
                words = x_banks.pop(s)[:]
            else:
                lo = 4 * (s % 2)
                words = x_by_k[s // 4, s % 4 // 2][:, lo : lo + 4, :]
            pairs = words.rearrange("p g c -> p (g c)").bitcast(BF16).rearrange("p (g c e) -> p g c e", g=4, e=2)
            maps = x1_by_k[:, s // 4, :].rearrange("p (c u e) -> p c u e", u=2, e=2)
            z1 = work.tile([P, CHUNK], BF16, name="z1", align_bytes=64, bufs=3)
            nc.vector.tensor_tensor(
                out=z1[:].rearrange("p (g c u e) -> p g c u e", g=4, u=2, e=2),
                in0=pairs.unsqueeze(3).to_broadcast([P, 4, P, 2, 2]),
                in1=maps.unsqueeze(1).to_broadcast([P, 4, P, 2, 2]),
                op=MULT,
            )
            return z1

        def leave_layer1(t, acc):
            nc.vector.tensor_tensor(
                out=o1[:, t, :].rearrange("p (u m e) -> p u m e", u=2, e=2),
                in0=acc[:].rearrange("p (m u e) -> p u m e", u=2, e=2),
                in1=b1_row[:].rearrange("p (m u e) -> p u m e", u=2, e=2),
                op=ADD,
            )
            if t > 0:
                before = o1[:, 0, :] if t == 1 else sums[:, 0:P]
                nc.gpsimd.tensor_tensor(out=sums[:, 0:P], in0=before, in1=o1[:, t, :], op=ADD)

        def make_z2(m):
            z2 = work.tile([P, 2, 16, 64], BF16, name="z2", bufs=3)
            source = o1[:, m // 4, :].rearrange("p (u c) -> p u c", u=2)
            share = vector_products(m)
            for r in range(16):
                i = 16 * (m % 4) + r
                scale = x_scale[:, m // 4, i : i + 1]
                if (r + 1) * share // 16 > r * share // 16:
                    nc.vector.tensor_scalar(out=z2[:, :, r, :], in0=source, scalar1=scale, scalar2=None, op0=MULT)
                else:
                    nc.scalar.activation(out=z2[:, :, r, :], in_=source, func=COPY, scale=scale)
            return z2

        def turn_z2(z2):
            words = z2[:].rearrange("p u r c -> p (u r c)").bitcast(F32)
            banks = []
            for half in range(2):
                bank = psum.tile([P, 2, 2, P], F32, name="bank", bufs=3)
                for g in range(2):
                    for u in range(2):
                        lo = 512 * u + 128 * (2 * half + g)
                        nc.tensor.transpose(bank[:, g, u, :], words[:, lo : lo + 128], ident[:])
                banks.append(bank)
            return banks

        def leave_banks(banks, m):
            z2_by_k = work.tile([P, CHUNK], BF16, name="z2_by_k", align_bytes=64, bufs=3)
            words = z2_by_k[:].bitcast(F32).rearrange("p (g c u) -> p g c u", g=4, u=2)
            for half in range(2):
                target = words[:, 2 * half : 2 * half + 2, :, :]
                source = banks[half][:].rearrange("p g u c -> p g c u")
                if m == CHUNKS - 1 and half == 0:
                    nc.vector.tensor_copy(out=target, in_=source)
                else:
                    nc.scalar.copy(out=target, in_=source)
            return z2_by_k

        def finish(layer):
            cols = slice(P * layer, P * layer + P)
            total = psum.tile([P, P], F32, name="bank", bufs=3)
            nc.tensor.matmul(total[:], lhsT=fold[:], rhs=sums[:, cols], start=True, stop=True)
            if layer == 0:
                nc.scalar.copy(
                    out=result[:, cols].rearrange("p (m u e) -> p m u e", u=2, e=2),
                    in_=total[:].rearrange("p (u m e) -> p m u e", u=2, e=2),
                )
            else:
                nc.vector.tensor_copy(out=result[:, cols], in_=total[:])
            nc.sync.dma_start(out=out[:, cols], in_=result[0:64, cols])

        turn_x1(1, 1)
        for s in range(1, 4):
            turn_x(s)

        acc1 = {}
        acc2 = psum.tile([P, P], F32, name="acc2")
        z1, z1_mx = {}, {}
        z2, z2_banks, z2_by_k, z2_mx = {}, {}, {}, {}
        w2_wide, w1_grouped, w2_grouped = {}, {}, {}

        for s in range(-1, CHUNKS + Z2_LAG + 4):
            m = s - Z2_LAG

            for pair in range(3):
                if X1_TURN_STEP[pair] == s:
                    turn_x1(2 * pair + 2, 2)
            if s == 2:
                nc.scalar.copy(out=x_scale[:], in_=x_by_tile[:, 0:TILES, :])
            for pair in range(3):
                if X_PARK_STEP[pair] == s:
                    park_x(pair + 1)
                    for t in (2 * pair + 2, 2 * pair + 3):
                        load_x(t, nc.sync, range(4))
            for n in range(4):
                if W2_WIDEN_STEP[n] == s:
                    w2_wide[n] = widen_w2(n)
            if s == 0:
                load_x(1, nc.scalar, (2, 3))
            for n in range(4):
                if W1_GROUP_STEP[n] == s:
                    w1_grouped[n] = group(w1_raw[n], W1_GROUP_ENGINE[n])

            if 0 <= m - 1 < CHUNKS:
                z2_banks[m - 1] = turn_z2(z2.pop(m - 1))
            done = s - MATMUL1_LAG
            if 0 <= done < CHUNKS:
                if done % 4 == 0:
                    acc1[done // 4] = psum.tile([P, P], F32, name="acc1", bufs=2)
                multiply(acc1[done // 4][:], z1_mx.pop(done), done, w1_codes, w1_scales, done % 4 == 0, done % 4 == 3)
            if 0 <= m - 3 < CHUNKS:
                multiply(acc2[:], z2_mx[m - 3], m - 3, w2_codes, w2_scales, m == 3, m - 3 == CHUNKS - 1)
                keep_clock(z2_mx.pop(m - 3))

            if 0 <= s < CHUNKS:
                z1[s] = make_z1(s)
            for n in range(4):
                if W2_GROUP_STEP[n] == s:
                    w2_grouped[n] = group(w2_wide.pop(n), W2_GROUP_ENGINE[n])
            if 0 <= m - 2 < CHUNKS:
                z2_mx[m - 2] = quantize(z2_by_k.pop(m - 2), "z2", 3)
            for n in range(4):
                if W1_QUANTIZE_STEP[n] == s:
                    quantize_weight(w1_grouped.pop(n), n, w1_codes, w1_scales)
                if W2_QUANTIZE_STEP[n] == s:
                    quantize_weight(w2_grouped.pop(n), n, w2_codes, w2_scales)
            if 0 <= m < CHUNKS:
                z2[m] = make_z2(m)
            if 0 <= m - 1 < CHUNKS:
                z2_by_k[m - 1] = leave_banks(z2_banks.pop(m - 1), m - 1)
            if 0 <= s < CHUNKS:
                z1_mx[s] = quantize(z1.pop(s), "z1", 8)
            if 0 <= done < CHUNKS and done % 4 == 3:
                leave_layer1(done // 4, acc1.pop(done // 4))
            if m == CHUNKS - 2:
                finish(0)

        nc.vector.scalar_tensor_tensor(
            out=sums[:, P : 2 * P], in0=b2_row[:], scalar=float(TILES), in1=acc2[:], op0=MULT, op1=ADD
        )
        finish(1)
